import numpy as np
import ml_dtypes


def mxq(x, axis, fmt="e4m3"):
    dtype, down = {"e4m3": (ml_dtypes.float8_e4m3fn, 7), "e5m2": (ml_dtypes.float8_e5m2, 14)}[fmt]
    v = np.moveaxis(np.asarray(x, np.float32).astype(ml_dtypes.bfloat16).astype(np.float64), axis, -1)
    blocks = v.reshape(v.shape[:-1] + (-1, 32))
    amax = np.abs(blocks).max(-1, keepdims=True)
    byte = np.maximum(np.where(amax > 0, np.frexp(amax)[1] - 1 + 127, 0) - down, 1)
    scale = np.exp2(byte - 127.0)
    codes = (blocks / scale).astype(np.float32).astype(dtype).astype(np.float64)
    return np.moveaxis((codes * scale).reshape(v.shape), -1, axis)


WIDE = False


def mx_kscale(k):
    if not WIDE:
        return np.ones(k)
    levels = np.array([10, -10, 5, -5, 0])
    a = np.random.permutation(np.resize(levels, k // 512 * 4)).reshape(k // 512, 4)
    idx = np.arange(k)
    return np.exp2(a[idx // 512, idx % 128 // 32])


BF16 = ml_dtypes.bfloat16


def bf(x):
    return np.asarray(x, np.float32).astype(BF16)


def f64(x):
    return np.asarray(x).astype(np.float64)


E2M1 = np.array([0.0, 0.5, 1.0, 1.5, 2.0, 3.0, 4.0, 6.0, -0.0, -0.5, -1.0, -1.5, -2.0, -3.0, -4.0, -6.0])


def pack_weight(w, fmt):
    k, n = w.shape
    w = f64(bf(w)).reshape(k // 32, 32, n)
    amax = np.abs(w).max(1)
    if fmt == "e4m3":
        byte = np.frexp(amax)[1] - 1 + 127 - 7
    else:
        mant, ex = np.frexp(amax / 6.0)
        byte = np.where(mant > 0.5, ex, ex - 1) + 127
    byte = np.clip(np.where(amax > 0, byte, 1), 1, 254)
    scaled = (w * np.exp2(127.0 - byte)[:, None, :]).reshape(k, n).astype(np.float32)
    by_word = np.ascontiguousarray(scaled.reshape(k // 512, 128, 4, n).transpose(0, 1, 3, 2))
    if fmt == "e4m3":
        words = by_word.astype(ml_dtypes.float8_e4m3fn).view(np.uint8)
    else:
        c = by_word.astype(ml_dtypes.float4_e2m1fn).view(np.uint8) & 0xF
        words = c[..., 0::2] | (c[..., 1::2] << 4)
    return np.ascontiguousarray(words), np.ascontiguousarray(byte.astype(np.uint8).reshape(k // 512, 16, n))


def unpack_weight(words, scales, fmt):
    g, p, n, _ = words.shape
    if fmt == "e4m3":
        vals = np.ascontiguousarray(words).view(ml_dtypes.float8_e4m3fn).astype(np.float64)
    else:
        nib = np.empty((g, p, n, 4), np.uint8)
        nib[..., 0::2] = words & 0xF
        nib[..., 1::2] = words >> 4
        vals = E2M1[nib]
    vals = vals * np.repeat(np.exp2(scales.astype(np.float64) - 127.0), 8, axis=1)[..., None]
    return vals.transpose(0, 1, 3, 2).reshape(g * 512, n)

def pack4(w):
    words, scales = pack_weight(w, "e2m1")
    return words.reshape(words.shape[0], 128, -1), scales


def unpack4(words, scales):
    return unpack_weight(words.reshape(words.shape[0], 128, -1, 2), scales, "e2m1")


B, S, D = 4, 512, 1024
NB = 2
W = 2 * NB + 1
LN_EPS = 1e-5


def setup_inputs():
    s = mx_kscale(D)
    u = s / s.max()
    pos = np.arange(S)[:, None] + np.arange(W)[None, :] - NB
    e = np.exp(np.random.standard_normal((B, S, W))) * ((pos >= 0) & (pos < S))
    x = bf(np.random.standard_normal((B, S, D)) * u)
    wv = np.random.standard_normal((D, D)) / np.sqrt(D) / u[None, :]
    words, scales = pack4(wv.T)
    return {"x": x,
            "Wv_words": words,
            "Wv_scales": scales,
            "bv": bf(0.2 + 0.2 * np.random.standard_normal(D)),
            "attn_band": bf(e / e.sum(-1, keepdims=True)),
            "gamma": bf(1.0 + 0.1 * np.random.standard_normal(D)),
            "beta": bf(0.2 * np.random.standard_normal(D))}


def reference(x, Wv_words, Wv_scales, bv, attn_band, gamma, beta):
    xf, a = f64(x), f64(attn_band)
    v = (mxq(xf, 2, "e4m3") @ unpack4(Wv_words, Wv_scales)) + f64(bv)
    mix = np.zeros_like(xf)
    for j in range(W):
        o = j - NB
        lo, hi = max(0, -o), S - max(0, o)
        mix[:, lo:hi] += a[:, lo:hi, j:j + 1] * v[:, lo + o:hi + o]
    out = mix + xf
    mu = out.mean(-1, keepdims=True)
    var = out.var(-1, keepdims=True)
    return (out - mu) / np.sqrt(var + LN_EPS) * f64(gamma) + f64(beta)

@@ -1,0 +1,176 @@
+from contextlib import ExitStack
+
+import concourse.masks as masks
+import concourse.mybir as mybir
+
+F32 = mybir.dt.float32
+BF16 = mybir.dt.bfloat16
+U8 = mybir.dt.uint8
+U32 = mybir.dt.uint32
+I32 = mybir.dt.int32
+FP8X4 = mybir.dt.float8_e4m3fn_x4
+FP4X4 = mybir.dt.float4_e2m1fn_x4
+ACT = mybir.ActivationFunctionType
+ALU = mybir.AluOpType
+
+P = 128
+D = 1024
+TOKENS = 4 * 512
+SETS = TOKENS // P
+CHUNK_SETS = 4
+CHUNKS = SETS // CHUNK_SETS
+CHUNK_TOKENS = CHUNK_SETS * P
+K_GROUPS = D // 512
+F_BLOCKS = D // P
+BANK = 512
+HALVES = D // BANK
+NB = 2
+TAPS = 2 * NB + 1
+LN_EPS = 1e-5
+
+FLOPS = 2 * TOKENS * D * D
+
+
+def tile_crosssliceattention_pb_kernel(tc, x, Wv_words, Wv_scales, bv, attn_band, gamma, beta, out):
+    nc = tc.nc
+    x_by_set = x.flatten_outer_dims().rearrange("(p r) d -> p r d", r=SETS)
+    out_by_set = out.flatten_outer_dims().rearrange("(p r) d -> p r d", r=SETS)
+
+    with ExitStack() as ctx:
+        keep = ctx.enter_context(tc.tile_pool(name="keep", bufs=1))
+        stage = ctx.enter_context(tc.tile_pool(name="stage", bufs=2))
+        stats = ctx.enter_context(tc.tile_pool(name="stats", bufs=4))
+        psum_xt = ctx.enter_context(tc.psum_pool(name="psum_xt", bufs=2))
+        psum_vt = ctx.enter_context(tc.psum_pool(name="psum_vt", bufs=2))
+        psum_vp = ctx.enter_context(tc.psum_pool(name="psum_vp", bufs=4))
+
+        ident = keep.tile([P, P], F32, name="ident")
+        masks.make_identity(nc, ident[:])
+        eps_col = keep.tile([P, 1], F32, name="eps_col")
+        nc.vector.memset(eps_col[:], LN_EPS)
+        w_scales = keep.tile([P, K_GROUPS, D], U8, name="w_scales", align_bytes=64)
+        nc.vector.memset(w_scales[:].rearrange("p g n -> p (g n)").bitcast(I32), 0)
+        bias_rows = keep.tile([P, P], F32, name="bias_rows")
+        nc.vector.memset(bias_rows[:], 0.0)
+
+        x_sb = [keep.tile([P, CHUNK_SETS, D], BF16, name="x_sb%d" % c) for c in range(CHUNKS)]
+
+        def load_x(c):
+            nc.sync.dma_start(out=x_sb[c][:], in_=x_by_set[:, CHUNK_SETS * c : CHUNK_SETS * (c + 1), :])
+
+        load_x(CHUNKS - 1)
+        for quad in range(4):
+            nc.sync.dma_start(
+                out=w_scales[32 * quad : 32 * quad + 4, :, :].bitcast(I32),
+                in_=Wv_scales[:, 4 * quad : 4 * quad + 4, :].rearrange("g r n -> r g n").bitcast(I32),
+            )
+        w_words = keep.tile([P, K_GROUPS, 2 * D], U8, name="w_words", align_bytes=64)
+        nc.sync.dma_start(out=w_words[:].bitcast(I32), in_=Wv_words.rearrange("g p n -> p g n").bitcast(I32))
+        bias_bf = keep.tile([F_BLOCKS, P], BF16, name="bias_bf")
+        nc.sync.dma_start(out=bias_bf[:], in_=bv.rearrange("(b f) -> b f", f=P))
+        load_x(0)
+        band_bf = keep.tile([P, SETS * TAPS], BF16, name="band_bf")
+        nc.sync.dma_start(out=band_bf[:], in_=attn_band.flatten_outer_dims().rearrange("(p r) j -> p (r j)", r=SETS))
+        load_x(1)
+        load_x(2)
+        gamma_bf = keep.tile([P, D], BF16, name="gamma_bf")
+        nc.sync.dma_start(out=gamma_bf[:], in_=gamma.partition_broadcast(P))
+        beta_bf = keep.tile([P, D], BF16, name="beta_bf")
+        nc.sync.dma_start(out=beta_bf[:], in_=beta.partition_broadcast(P))
+
+        nc.vector.tensor_copy(out=bias_rows[0:F_BLOCKS, :], in_=bias_bf[:])
+        bias_ps = psum_xt.tile([P, P], F32, name="bias_ps", tag="xt")
+        nc.tensor.transpose(bias_ps[:], bias_rows[:], ident[:])
+        bias_col = keep.tile([P, F_BLOCKS], F32, name="bias_col")
+        nc.vector.tensor_copy(out=bias_col[:], in_=bias_ps[:, 0:F_BLOCKS])
+        band = keep.tile([P, SETS * TAPS], F32, name="band")
+        nc.vector.tensor_copy(out=band[:], in_=band_bf[:])
+        gamma_f = keep.tile([P, D], F32, name="gamma_f")
+        nc.gpsimd.tensor_scalar(out=gamma_f[:], in0=gamma_bf[:], scalar1=1.0, scalar2=0.0, op0=ALU.mult, op1=ALU.add)
+        beta_f = keep.tile([P, D], F32, name="beta_f")
+        nc.gpsimd.tensor_scalar(out=beta_f[:], in0=beta_bf[:], scalar1=1.0, scalar2=0.0, op0=ALU.mult, op1=ALU.add)
+
+        vbT = [keep.tile([P, F_BLOCKS, CHUNK_TOKENS], F32, name="vbT%d" % c) for c in range(CHUNKS)]
+        acc = [keep.tile([P, D], F32, name="acc%d" % d) for d in range(SETS)]
+        row_sums = [keep.tile([P, HALVES], F32, name="row_sums%d" % d) for d in range(SETS)]
+
+        def project_chunk(c):
+            x_words = x_sb[c][:].bitcast(F32)
+            grouped = stage.tile([P, K_GROUPS, CHUNK_TOKENS, 4], BF16, name="grouped", align_bytes=64)
+            grouped_words = grouped[:].bitcast(F32)
+            for i in range(CHUNK_SETS):
+                xt = psum_xt.tile([P, K_GROUPS, 2, P], F32, name="xt", tag="xt")
+                for g in range(K_GROUPS):
+                    for u in range(2):
+                        nc.tensor.transpose(xt[:, g, u, :], x_words[:, i, 256 * g + u : 256 * (g + 1) : 2], ident[:])
+                nc.scalar.copy(
+                    out=grouped_words[:, :, P * i : P * (i + 1), :], in_=xt[:].rearrange("q g u t -> q g t u")
+                )
+            x_codes = stage.tile([P, K_GROUPS, CHUNK_TOKENS], U32, name="x_codes", align_bytes=64)
+            x_scales = stage.tile([P, K_GROUPS, CHUNK_TOKENS], U8, name="x_scales", align_bytes=64)
+            nc.vector.quantize_mx(
+                out=x_codes[:].rearrange("q g t -> q (g t)").bitcast(FP8X4),
+                scales=x_scales[:].rearrange("q g t -> q (g t)"),
+                in_=grouped[:].rearrange("q g t j -> q (g t j)"),
+            )
+            for b in range(F_BLOCKS):
+                vt = psum_vt.tile([P, CHUNK_TOKENS], F32, name="vt")
+                for g in range(K_GROUPS):
+                    nc.tensor.matmul_mx(
+                        out=vt[:],
+                        lhsT=w_words[:, g, 2 * P * b : 2 * P * (b + 1)].bitcast(FP4X4),
+                        lhsT_scale=w_scales[:, g, P * b : P * (b + 1)],
+                        rhs=x_codes[:, g, :].bitcast(FP8X4),
+                        rhs_scale=x_scales[:, g, :],
+                        start=(g == 0),
+                        stop=(g == K_GROUPS - 1),
+                    )
+                nc.scalar.activation(out=vbT[c][:, b, :], in_=vt[:], func=ACT.Identity, bias=bias_col[:, b : b + 1], scale=1.0)
+
+        def spread_set(r):
+            c = (r % SETS) // CHUNK_SETS
+            first = ((r % SETS) % CHUNK_SETS) * P + r // SETS
+            for h in range(HALVES):
+                cols = slice(BANK * h, BANK * (h + 1))
+                vp = psum_vp.tile([P, BANK], F32, name="vp")
+                for q in range(BANK // P):
+                    nc.tensor.transpose(
+                        vp[:, P * q : P * (q + 1)], vbT[c][:, (BANK // P) * h + q, first : first + P], ident[:]
+                    )
+                for d in range(max(r - NB, 0), min(r + NB, SETS - 1) + 1):
+                    j = r - d + NB
+                    before = x_sb[d // CHUNK_SETS][:, d % CHUNK_SETS, cols] if j == 0 else acc[d][:, cols]
+                    nc.vector.scalar_tensor_tensor(
+                        out=acc[d][:, cols],
+                        in0=vp[:],
+                        scalar=band[:, TAPS * d + j : TAPS * d + j + 1],
+                        in1=before,
+                        op0=ALU.mult,
+                        op1=ALU.add,
+                        accum_out=row_sums[d][:, h : h + 1] if j == TAPS - 1 else None,
+                    )
+
+        def normalise_set(d):
+            halves = stats.tile([P, HALVES], F32, name="halves")
+            neg_mean = stats.tile([P, 1], F32, name="neg_mean")
+            nc.scalar.activation(out=halves[:], in_=row_sums[d][:], func=ACT.Identity, scale=-1.0 / D, accum_out=neg_mean[:])
+            squares = stage.tile([P, D], BF16, name="squares")
+            sum_sq = stats.tile([P, 1], F32, name="sum_sq")
+            nc.scalar.activation(out=squares[:], in_=acc[d][:], func=ACT.Square, bias=neg_mean[:], scale=1.0, accum_out=sum_sq[:])
+            rstd = stats.tile([P, 1], F32, name="rstd")
+            nc.scalar.activation(out=rstd[:], in_=sum_sq[:], func=ACT.Abs_reciprocal_sqrt, bias=eps_col[:], scale=1.0 / D)
+            shift = stats.tile([P, 1], F32, name="shift")
+            nc.scalar.activation(out=shift[:], in_=neg_mean[:], func=ACT.Copy, scale=rstd[:])
+            nc.scalar.activation(out=acc[d][:], in_=acc[d][:], func=ACT.Identity, bias=shift[:], scale=rstd[:])
+            nc.gpsimd.tensor_tensor(out=acc[d][:], in0=acc[d][:], in1=gamma_f[:], op=ALU.mult)
+            nc.gpsimd.tensor_tensor(out=acc[d][:], in0=acc[d][:], in1=beta_f[:], op=ALU.add)
+            nc.sync.dma_start(out=out_by_set[:, d, :], in_=acc[d][:])
+
+        project_chunk(CHUNKS - 1)
+        project_chunk(0)
+        for r in range(-NB, SETS + NB):
+            if r % CHUNK_SETS == 0 and 0 <= r // CHUNK_SETS < CHUNKS - 2:
+                project_chunk(r // CHUNK_SETS + 1)
+            spread_set(r)
+            if r - NB >= 0:
+                normalise_set(r - NB)

@@ -36,13 +36,16 @@ def tile_crosssliceattention_pb_kernel(tc, x, Wv_words, Wv_scales, bv, attn_band
     x_by_set = x.flatten_outer_dims().rearrange("(p r) d -> p r d", r=SETS)
     out_by_set = out.flatten_outer_dims().rearrange("(p r) d -> p r d", r=SETS)
 
+    chunk_order = [0, CHUNKS - 1] + list(range(1, CHUNKS - 1))
+    set_order = list(range(CHUNK_SETS)) + list(range(-NB, 0)) + list(range(CHUNK_SETS, SETS + NB))
+
     with ExitStack() as ctx:
         keep = ctx.enter_context(tc.tile_pool(name="keep", bufs=1))
         stage = ctx.enter_context(tc.tile_pool(name="stage", bufs=2))
         stats = ctx.enter_context(tc.tile_pool(name="stats", bufs=4))
         psum_xt = ctx.enter_context(tc.psum_pool(name="psum_xt", bufs=2))
         psum_vt = ctx.enter_context(tc.psum_pool(name="psum_vt", bufs=2))
-        psum_vp = ctx.enter_context(tc.psum_pool(name="psum_vp", bufs=4))
+        psum_vp = ctx.enter_context(tc.psum_pool(name="psum_vp", bufs=2 * HALVES))
 
         ident = keep.tile([P, P], F32, name="ident")
         masks.make_identity(nc, ident[:])
@@ -53,12 +56,13 @@ def tile_crosssliceattention_pb_kernel(tc, x, Wv_words, Wv_scales, bv, attn_band
         bias_rows = keep.tile([P, P], F32, name="bias_rows")
         nc.vector.memset(bias_rows[:], 0.0)
 
-        x_sb = [keep.tile([P, CHUNK_SETS, D], BF16, name="x_sb%d" % c) for c in range(CHUNKS)]
+        x_sb = [keep.tile([P, D], BF16, name="x_sb%d" % r) for r in range(SETS)]
 
-        def load_x(c):
-            nc.sync.dma_start(out=x_sb[c][:], in_=x_by_set[:, CHUNK_SETS * c : CHUNK_SETS * (c + 1), :])
+        def load_chunk(c):
+            for r in range(CHUNK_SETS * c, CHUNK_SETS * (c + 1)):
+                nc.sync.dma_start(out=x_sb[r][:], in_=x_by_set[:, r, :])
 
-        load_x(CHUNKS - 1)
+        load_chunk(chunk_order[0])
         for quad in range(4):
             nc.sync.dma_start(
                 out=w_scales[32 * quad : 32 * quad + 4, :, :].bitcast(I32),
@@ -68,11 +72,10 @@ def tile_crosssliceattention_pb_kernel(tc, x, Wv_words, Wv_scales, bv, attn_band
         nc.sync.dma_start(out=w_words[:].bitcast(I32), in_=Wv_words.rearrange("g p n -> p g n").bitcast(I32))
         bias_bf = keep.tile([F_BLOCKS, P], BF16, name="bias_bf")
         nc.sync.dma_start(out=bias_bf[:], in_=bv.rearrange("(b f) -> b f", f=P))
-        load_x(0)
         band_bf = keep.tile([P, SETS * TAPS], BF16, name="band_bf")
         nc.sync.dma_start(out=band_bf[:], in_=attn_band.flatten_outer_dims().rearrange("(p r) j -> p (r j)", r=SETS))
-        load_x(1)
-        load_x(2)
+        for c in chunk_order[1:]:
+            load_chunk(c)
         gamma_bf = keep.tile([P, D], BF16, name="gamma_bf")
         nc.sync.dma_start(out=gamma_bf[:], in_=gamma.partition_broadcast(P))
         beta_bf = keep.tile([P, D], BF16, name="beta_bf")
@@ -93,26 +96,37 @@ def tile_crosssliceattention_pb_kernel(tc, x, Wv_words, Wv_scales, bv, attn_band
         vbT = [keep.tile([P, F_BLOCKS, CHUNK_TOKENS], F32, name="vbT%d" % c) for c in range(CHUNKS)]
         acc = [keep.tile([P, D], F32, name="acc%d" % d) for d in range(SETS)]
         row_sums = [keep.tile([P, HALVES], F32, name="row_sums%d" % d) for d in range(SETS)]
+        taps_added = [0] * SETS
+        grouped_of = {}
+        quantised_of = {}
+        rows_of = {}
 
-        def project_chunk(c):
-            x_words = x_sb[c][:].bitcast(F32)
+        def transpose_chunk(c):
             grouped = stage.tile([P, K_GROUPS, CHUNK_TOKENS, 4], BF16, name="grouped", align_bytes=64)
             grouped_words = grouped[:].bitcast(F32)
             for i in range(CHUNK_SETS):
+                x_words = x_sb[CHUNK_SETS * c + i][:].bitcast(F32)
                 xt = psum_xt.tile([P, K_GROUPS, 2, P], F32, name="xt", tag="xt")
                 for g in range(K_GROUPS):
                     for u in range(2):
-                        nc.tensor.transpose(xt[:, g, u, :], x_words[:, i, 256 * g + u : 256 * (g + 1) : 2], ident[:])
+                        nc.tensor.transpose(xt[:, g, u, :], x_words[:, 256 * g + u : 256 * (g + 1) : 2], ident[:])
                 nc.scalar.copy(
                     out=grouped_words[:, :, P * i : P * (i + 1), :], in_=xt[:].rearrange("q g u t -> q g t u")
                 )
+            grouped_of[c] = grouped
+
+        def quantise_chunk(c):
             x_codes = stage.tile([P, K_GROUPS, CHUNK_TOKENS], U32, name="x_codes", align_bytes=64)
             x_scales = stage.tile([P, K_GROUPS, CHUNK_TOKENS], U8, name="x_scales", align_bytes=64)
             nc.vector.quantize_mx(
                 out=x_codes[:].rearrange("q g t -> q (g t)").bitcast(FP8X4),
                 scales=x_scales[:].rearrange("q g t -> q (g t)"),
-                in_=grouped[:].rearrange("q g t j -> q (g t j)"),
+                in_=grouped_of[c][:].rearrange("q g t j -> q (g t j)"),
             )
+            quantised_of[c] = (x_codes, x_scales)
+
+        def multiply_chunk(c):
+            x_codes, x_scales = quantised_of[c]
             for b in range(F_BLOCKS):
                 vt = psum_vt.tile([P, CHUNK_TOKENS], F32, name="vt")
                 for g in range(K_GROUPS):
@@ -127,28 +141,36 @@ def tile_crosssliceattention_pb_kernel(tc, x, Wv_words, Wv_scales, bv, attn_band
                     )
                 nc.scalar.activation(out=vbT[c][:, b, :], in_=vt[:], func=ACT.Identity, bias=bias_col[:, b : b + 1], scale=1.0)
 
-        def spread_set(r):
+        def transpose_back(r):
             c = (r % SETS) // CHUNK_SETS
             first = ((r % SETS) % CHUNK_SETS) * P + r // SETS
+            rows_of[r] = []
             for h in range(HALVES):
-                cols = slice(BANK * h, BANK * (h + 1))
                 vp = psum_vp.tile([P, BANK], F32, name="vp")
                 for q in range(BANK // P):
                     nc.tensor.transpose(
                         vp[:, P * q : P * (q + 1)], vbT[c][:, (BANK // P) * h + q, first : first + P], ident[:]
                     )
-                for d in range(max(r - NB, 0), min(r + NB, SETS - 1) + 1):
+                rows_of[r].append(vp)
+
+        def add_taps(r):
+            dests = range(max(r - NB, 0), min(r + NB, SETS - 1) + 1)
+            for h in range(HALVES):
+                cols = slice(BANK * h, BANK * (h + 1))
+                for d in dests:
                     j = r - d + NB
-                    before = x_sb[d // CHUNK_SETS][:, d % CHUNK_SETS, cols] if j == 0 else acc[d][:, cols]
                     nc.vector.scalar_tensor_tensor(
                         out=acc[d][:, cols],
-                        in0=vp[:],
+                        in0=rows_of[r][h][:],
                         scalar=band[:, TAPS * d + j : TAPS * d + j + 1],
-                        in1=before,
+                        in1=x_sb[d][:, cols] if taps_added[d] == 0 else acc[d][:, cols],
                         op0=ALU.mult,
                         op1=ALU.add,
-                        accum_out=row_sums[d][:, h : h + 1] if j == TAPS - 1 else None,
+                        accum_out=row_sums[d][:, h : h + 1] if taps_added[d] == TAPS - 1 else None,
                     )
+            for d in dests:
+                taps_added[d] += 1
+            return [d for d in dests if taps_added[d] == TAPS]
 
         def normalise_set(d):
             halves = stats.tile([P, HALVES], F32, name="halves")
@@ -159,18 +181,35 @@ def tile_crosssliceattention_pb_kernel(tc, x, Wv_words, Wv_scales, bv, attn_band
             nc.scalar.activation(out=squares[:], in_=acc[d][:], func=ACT.Square, bias=neg_mean[:], scale=1.0, accum_out=sum_sq[:])
             rstd = stats.tile([P, 1], F32, name="rstd")
             nc.scalar.activation(out=rstd[:], in_=sum_sq[:], func=ACT.Abs_reciprocal_sqrt, bias=eps_col[:], scale=1.0 / D)
-            shift = stats.tile([P, 1], F32, name="shift")
-            nc.scalar.activation(out=shift[:], in_=neg_mean[:], func=ACT.Copy, scale=rstd[:])
-            nc.scalar.activation(out=acc[d][:], in_=acc[d][:], func=ACT.Identity, bias=shift[:], scale=rstd[:])
-            nc.gpsimd.tensor_tensor(out=acc[d][:], in0=acc[d][:], in1=gamma_f[:], op=ALU.mult)
-            nc.gpsimd.tensor_tensor(out=acc[d][:], in0=acc[d][:], in1=beta_f[:], op=ALU.add)
+            if d < SETS - NB:
+                shift = stats.tile([P, 1], F32, name="shift")
+                nc.scalar.activation(out=shift[:], in_=neg_mean[:], func=ACT.Copy, scale=rstd[:])
+                nc.scalar.activation(out=acc[d][:], in_=acc[d][:], func=ACT.Identity, bias=shift[:], scale=rstd[:])
+                nc.gpsimd.tensor_tensor(out=acc[d][:], in0=acc[d][:], in1=gamma_f[:], op=ALU.mult)
+                nc.gpsimd.tensor_tensor(out=acc[d][:], in0=acc[d][:], in1=beta_f[:], op=ALU.add)
+            else:
+                nc.vector.scalar_tensor_tensor(
+                    out=acc[d][:], in0=acc[d][:], scalar=neg_mean[:], in1=gamma_f[:], op0=ALU.add, op1=ALU.mult
+                )
+                nc.vector.scalar_tensor_tensor(
+                    out=acc[d][:], in0=acc[d][:], scalar=rstd[:], in1=beta_f[:], op0=ALU.mult, op1=ALU.add
+                )
             nc.sync.dma_start(out=out_by_set[:, d, :], in_=acc[d][:])
 
-        project_chunk(CHUNKS - 1)
-        project_chunk(0)
-        for r in range(-NB, SETS + NB):
-            if r % CHUNK_SETS == 0 and 0 <= r // CHUNK_SETS < CHUNKS - 2:
-                project_chunk(r // CHUNK_SETS + 1)
-            spread_set(r)
-            if r - NB >= 0:
-                normalise_set(r - NB)
+        transpose_chunk(chunk_order[0])
+        quantise_chunk(chunk_order[0])
+        multiply_chunk(chunk_order[0])
+        transpose_back(set_order[0])
+        for step, r in enumerate(set_order):
+            if step + 1 < len(set_order):
+                transpose_back(set_order[step + 1])
+            later = chunk_order[1 + r // 2] if 0 <= r < 2 * (CHUNKS - 1) else None
+            if later is not None and r % 2 == 0:
+                transpose_chunk(later)
+            if later is not None and r % 2 == 1:
+                multiply_chunk(later)
+            finished = add_taps(r)
+            if later is not None and r % 2 == 0:
+                quantise_chunk(later)
+            for d in finished:
+                normalise_set(d)

@@ -36,8 +36,8 @@ def tile_crosssliceattention_pb_kernel(tc, x, Wv_words, Wv_scales, bv, attn_band
     x_by_set = x.flatten_outer_dims().rearrange("(p r) d -> p r d", r=SETS)
     out_by_set = out.flatten_outer_dims().rearrange("(p r) d -> p r d", r=SETS)
 
-    chunk_order = [0, CHUNKS - 1] + list(range(1, CHUNKS - 1))
-    set_order = list(range(CHUNK_SETS)) + list(range(-NB, 0)) + list(range(CHUNK_SETS, SETS + NB))
+    chunk_order = [0, 1, CHUNKS - 1, 2]
+    set_order = list(range(2 * CHUNK_SETS)) + list(range(-NB, 0)) + list(range(2 * CHUNK_SETS, SETS + NB))
 
     with ExitStack() as ctx:
         keep = ctx.enter_context(tc.tile_pool(name="keep", bufs=1))
@@ -58,11 +58,15 @@ def tile_crosssliceattention_pb_kernel(tc, x, Wv_words, Wv_scales, bv, attn_band
 
         x_sb = [keep.tile([P, D], BF16, name="x_sb%d" % r) for r in range(SETS)]
 
-        def load_chunk(c):
-            for r in range(CHUNK_SETS * c, CHUNK_SETS * (c + 1)):
+        def load_sets(sets):
+            for r in sets:
                 nc.sync.dma_start(out=x_sb[r][:], in_=x_by_set[:, r, :])
 
-        load_chunk(chunk_order[0])
+        bias_bf = keep.tile([F_BLOCKS, P], BF16, name="bias_bf")
+        nc.sync.dma_start(out=bias_bf[:], in_=bv.rearrange("(b f) -> b f", f=P))
+        band_bf = keep.tile([P, SETS * TAPS], BF16, name="band_bf")
+        nc.sync.dma_start(out=band_bf[:], in_=attn_band.flatten_outer_dims().rearrange("(p r) j -> p (r j)", r=SETS))
+        load_sets(range(1))
         for quad in range(4):
             nc.sync.dma_start(
                 out=w_scales[32 * quad : 32 * quad + 4, :, :].bitcast(I32),
@@ -70,12 +74,9 @@ def tile_crosssliceattention_pb_kernel(tc, x, Wv_words, Wv_scales, bv, attn_band
             )
         w_words = keep.tile([P, K_GROUPS, 2 * D], U8, name="w_words", align_bytes=64)
         nc.sync.dma_start(out=w_words[:].bitcast(I32), in_=Wv_words.rearrange("g p n -> p g n").bitcast(I32))
-        bias_bf = keep.tile([F_BLOCKS, P], BF16, name="bias_bf")
-        nc.sync.dma_start(out=bias_bf[:], in_=bv.rearrange("(b f) -> b f", f=P))
-        band_bf = keep.tile([P, SETS * TAPS], BF16, name="band_bf")
-        nc.sync.dma_start(out=band_bf[:], in_=attn_band.flatten_outer_dims().rearrange("(p r) j -> p (r j)", r=SETS))
+        load_sets(range(1, CHUNK_SETS))
         for c in chunk_order[1:]:
-            load_chunk(c)
+            load_sets(range(CHUNK_SETS * c, CHUNK_SETS * (c + 1)))
         gamma_bf = keep.tile([P, D], BF16, name="gamma_bf")
         nc.sync.dma_start(out=gamma_bf[:], in_=gamma.partition_broadcast(P))
         beta_bf = keep.tile([P, D], BF16, name="beta_bf")
@@ -98,13 +99,23 @@ def tile_crosssliceattention_pb_kernel(tc, x, Wv_words, Wv_scales, bv, attn_band
         row_sums = [keep.tile([P, HALVES], F32, name="row_sums%d" % d) for d in range(SETS)]
         taps_added = [0] * SETS
         grouped_of = {}
-        quantised_of = {}
+        codes_of = {}
+        scales_of = {}
         rows_of = {}
 
-        def transpose_chunk(c):
-            grouped = stage.tile([P, K_GROUPS, CHUNK_TOKENS, 4], BF16, name="grouped", align_bytes=64)
-            grouped_words = grouped[:].bitcast(F32)
-            for i in range(CHUNK_SETS):
+        def begin_chunk(c):
+            grouped_of[c] = stage.tile([P, K_GROUPS, CHUNK_TOKENS, 4], BF16, name="grouped", align_bytes=64)
+            codes_of[c] = stage.tile([P, K_GROUPS, CHUNK_TOKENS], U32, name="x_codes", align_bytes=64)
+            scales_of[c] = stage.tile([P, K_GROUPS, CHUNK_TOKENS], U8, name="x_scales", align_bytes=64)
+
+        def project_sets(c, sets):
+            transpose_sets(c, sets)
+            quantise_sets(c, sets)
+            multiply_sets(c, sets)
+
+        def transpose_sets(c, sets):
+            grouped_words = grouped_of[c][:].bitcast(F32)
+            for i in sets:
                 x_words = x_sb[CHUNK_SETS * c + i][:].bitcast(F32)
                 xt = psum_xt.tile([P, K_GROUPS, 2, P], F32, name="xt", tag="xt")
                 for g in range(K_GROUPS):
@@ -113,33 +124,33 @@ def tile_crosssliceattention_pb_kernel(tc, x, Wv_words, Wv_scales, bv, attn_band
                 nc.scalar.copy(
                     out=grouped_words[:, :, P * i : P * (i + 1), :], in_=xt[:].rearrange("q g u t -> q g t u")
                 )
-            grouped_of[c] = grouped
 
-        def quantise_chunk(c):
-            x_codes = stage.tile([P, K_GROUPS, CHUNK_TOKENS], U32, name="x_codes", align_bytes=64)
-            x_scales = stage.tile([P, K_GROUPS, CHUNK_TOKENS], U8, name="x_scales", align_bytes=64)
-            nc.vector.quantize_mx(
-                out=x_codes[:].rearrange("q g t -> q (g t)").bitcast(FP8X4),
-                scales=x_scales[:].rearrange("q g t -> q (g t)"),
-                in_=grouped_of[c][:].rearrange("q g t j -> q (g t j)"),
-            )
-            quantised_of[c] = (x_codes, x_scales)
+        def quantise_sets(c, sets):
+            tokens = slice(P * sets[0], P * (sets[-1] + 1))
+            for g in range(K_GROUPS):
+                nc.vector.quantize_mx(
+                    out=codes_of[c][:, g, tokens].bitcast(FP8X4),
+                    scales=scales_of[c][:, g, tokens],
+                    in_=grouped_of[c][:, g, tokens, :].rearrange("q t j -> q (t j)"),
+                )
 
-        def multiply_chunk(c):
-            x_codes, x_scales = quantised_of[c]
+        def multiply_sets(c, sets):
+            tokens = slice(P * sets[0], P * (sets[-1] + 1))
             for b in range(F_BLOCKS):
-                vt = psum_vt.tile([P, CHUNK_TOKENS], F32, name="vt")
+                vt = psum_vt.tile([P, P * len(sets)], F32, name="vt")
                 for g in range(K_GROUPS):
                     nc.tensor.matmul_mx(
                         out=vt[:],
                         lhsT=w_words[:, g, 2 * P * b : 2 * P * (b + 1)].bitcast(FP4X4),
                         lhsT_scale=w_scales[:, g, P * b : P * (b + 1)],
-                        rhs=x_codes[:, g, :].bitcast(FP8X4),
-                        rhs_scale=x_scales[:, g, :],
+                        rhs=codes_of[c][:, g, tokens].bitcast(FP8X4),
+                        rhs_scale=scales_of[c][:, g, tokens],
                         start=(g == 0),
                         stop=(g == K_GROUPS - 1),
                     )
-                nc.scalar.activation(out=vbT[c][:, b, :], in_=vt[:], func=ACT.Identity, bias=bias_col[:, b : b + 1], scale=1.0)
+                nc.scalar.activation(
+                    out=vbT[c][:, b, tokens], in_=vt[:], func=ACT.Identity, bias=bias_col[:, b : b + 1], scale=1.0
+                )
 
         def transpose_back(r):
             c = (r % SETS) // CHUNK_SETS
@@ -196,20 +207,14 @@ def tile_crosssliceattention_pb_kernel(tc, x, Wv_words, Wv_scales, bv, attn_band
                 )
             nc.sync.dma_start(out=out_by_set[:, d, :], in_=acc[d][:])
 
-        transpose_chunk(chunk_order[0])
-        quantise_chunk(chunk_order[0])
-        multiply_chunk(chunk_order[0])
-        transpose_back(set_order[0])
-        for step, r in enumerate(set_order):
-            if step + 1 < len(set_order):
-                transpose_back(set_order[step + 1])
-            later = chunk_order[1 + r // 2] if 0 <= r < 2 * (CHUNKS - 1) else None
-            if later is not None and r % 2 == 0:
-                transpose_chunk(later)
-            if later is not None and r % 2 == 1:
-                multiply_chunk(later)
-            finished = add_taps(r)
-            if later is not None and r % 2 == 0:
-                quantise_chunk(later)
-            for d in finished:
+        begin_chunk(chunk_order[0])
+        for i in range(CHUNK_SETS):
+            project_sets(chunk_order[0], [i])
+        for c in chunk_order[1:]:
+            begin_chunk(c)
+            project_sets(c, list(range(CHUNK_SETS)))
+        for r in set_order:
+            with tc.high_priority():
+                transpose_back(r)
+            for d in add_taps(r):
                 normalise_set(d)

@@ -36,8 +36,8 @@ def tile_crosssliceattention_pb_kernel(tc, x, Wv_words, Wv_scales, bv, attn_band
     x_by_set = x.flatten_outer_dims().rearrange("(p r) d -> p r d", r=SETS)
     out_by_set = out.flatten_outer_dims().rearrange("(p r) d -> p r d", r=SETS)
 
-    chunk_order = [0, 1, CHUNKS - 1, 2]
-    set_order = list(range(2 * CHUNK_SETS)) + list(range(-NB, 0)) + list(range(2 * CHUNK_SETS, SETS + NB))
+    chunk_order = [0, CHUNKS - 1] + list(range(1, CHUNKS - 1))
+    set_order = list(range(CHUNK_SETS)) + list(range(-NB, 0)) + list(range(CHUNK_SETS, SETS + NB))
 
     with ExitStack() as ctx:
         keep = ctx.enter_context(tc.tile_pool(name="keep", bufs=1))
@@ -51,6 +51,8 @@ def tile_crosssliceattention_pb_kernel(tc, x, Wv_words, Wv_scales, bv, attn_band
         masks.make_identity(nc, ident[:])
         eps_col = keep.tile([P, 1], F32, name="eps_col")
         nc.vector.memset(eps_col[:], LN_EPS)
+        warm = keep.tile([P, 1], F32, name="warm")
+        nc.scalar.activation(out=warm[:], in_=eps_col[:], func=ACT.Abs_reciprocal_sqrt)
         w_scales = keep.tile([P, K_GROUPS, D], U8, name="w_scales", align_bytes=64)
         nc.vector.memset(w_scales[:].rearrange("p g n -> p (g n)").bitcast(I32), 0)
         bias_rows = keep.tile([P, P], F32, name="bias_rows")
@@ -58,15 +60,13 @@ def tile_crosssliceattention_pb_kernel(tc, x, Wv_words, Wv_scales, bv, attn_band
 
         x_sb = [keep.tile([P, D], BF16, name="x_sb%d" % r) for r in range(SETS)]
 
-        def load_sets(sets):
-            for r in sets:
+        def load_chunk(c):
+            for r in range(CHUNK_SETS * c, CHUNK_SETS * (c + 1)):
                 nc.sync.dma_start(out=x_sb[r][:], in_=x_by_set[:, r, :])
 
         bias_bf = keep.tile([F_BLOCKS, P], BF16, name="bias_bf")
         nc.sync.dma_start(out=bias_bf[:], in_=bv.rearrange("(b f) -> b f", f=P))
-        band_bf = keep.tile([P, SETS * TAPS], BF16, name="band_bf")
-        nc.sync.dma_start(out=band_bf[:], in_=attn_band.flatten_outer_dims().rearrange("(p r) j -> p (r j)", r=SETS))
-        load_sets(range(1))
+        load_chunk(chunk_order[0])
         for quad in range(4):
             nc.sync.dma_start(
                 out=w_scales[32 * quad : 32 * quad + 4, :, :].bitcast(I32),
@@ -74,9 +74,10 @@ def tile_crosssliceattention_pb_kernel(tc, x, Wv_words, Wv_scales, bv, attn_band
             )
         w_words = keep.tile([P, K_GROUPS, 2 * D], U8, name="w_words", align_bytes=64)
         nc.sync.dma_start(out=w_words[:].bitcast(I32), in_=Wv_words.rearrange("g p n -> p g n").bitcast(I32))
-        load_sets(range(1, CHUNK_SETS))
+        band_bf = keep.tile([P, SETS * TAPS], BF16, name="band_bf")
+        nc.sync.dma_start(out=band_bf[:], in_=attn_band.flatten_outer_dims().rearrange("(p r) j -> p (r j)", r=SETS))
         for c in chunk_order[1:]:
-            load_sets(range(CHUNK_SETS * c, CHUNK_SETS * (c + 1)))
+            load_chunk(c)
         gamma_bf = keep.tile([P, D], BF16, name="gamma_bf")
         nc.sync.dma_start(out=gamma_bf[:], in_=gamma.partition_broadcast(P))
         beta_bf = keep.tile([P, D], BF16, name="beta_bf")
@@ -97,25 +98,14 @@ def tile_crosssliceattention_pb_kernel(tc, x, Wv_words, Wv_scales, bv, attn_band
         vbT = [keep.tile([P, F_BLOCKS, CHUNK_TOKENS], F32, name="vbT%d" % c) for c in range(CHUNKS)]
         acc = [keep.tile([P, D], F32, name="acc%d" % d) for d in range(SETS)]
         row_sums = [keep.tile([P, HALVES], F32, name="row_sums%d" % d) for d in range(SETS)]
-        taps_added = [0] * SETS
+        taps_added = [[0] * SETS for h in range(HALVES)]
         grouped_of = {}
-        codes_of = {}
-        scales_of = {}
-        rows_of = {}
+        quantised_of = {}
 
-        def begin_chunk(c):
-            grouped_of[c] = stage.tile([P, K_GROUPS, CHUNK_TOKENS, 4], BF16, name="grouped", align_bytes=64)
-            codes_of[c] = stage.tile([P, K_GROUPS, CHUNK_TOKENS], U32, name="x_codes", align_bytes=64)
-            scales_of[c] = stage.tile([P, K_GROUPS, CHUNK_TOKENS], U8, name="x_scales", align_bytes=64)
-
-        def project_sets(c, sets):
-            transpose_sets(c, sets)
-            quantise_sets(c, sets)
-            multiply_sets(c, sets)
-
-        def transpose_sets(c, sets):
-            grouped_words = grouped_of[c][:].bitcast(F32)
-            for i in sets:
+        def transpose_chunk(c):
+            grouped = stage.tile([P, K_GROUPS, CHUNK_TOKENS, 4], BF16, name="grouped", align_bytes=64)
+            grouped_words = grouped[:].bitcast(F32)
+            for i in range(CHUNK_SETS):
                 x_words = x_sb[CHUNK_SETS * c + i][:].bitcast(F32)
                 xt = psum_xt.tile([P, K_GROUPS, 2, P], F32, name="xt", tag="xt")
                 for g in range(K_GROUPS):
@@ -124,64 +114,55 @@ def tile_crosssliceattention_pb_kernel(tc, x, Wv_words, Wv_scales, bv, attn_band
                 nc.scalar.copy(
                     out=grouped_words[:, :, P * i : P * (i + 1), :], in_=xt[:].rearrange("q g u t -> q g t u")
                 )
+            grouped_of[c] = grouped
 
-        def quantise_sets(c, sets):
-            tokens = slice(P * sets[0], P * (sets[-1] + 1))
-            for g in range(K_GROUPS):
-                nc.vector.quantize_mx(
-                    out=codes_of[c][:, g, tokens].bitcast(FP8X4),
-                    scales=scales_of[c][:, g, tokens],
-                    in_=grouped_of[c][:, g, tokens, :].rearrange("q t j -> q (t j)"),
-                )
+        def quantise_chunk(c):
+            x_codes = stage.tile([P, K_GROUPS, CHUNK_TOKENS], U32, name="x_codes", align_bytes=64)
+            x_scales = stage.tile([P, K_GROUPS, CHUNK_TOKENS], U8, name="x_scales", align_bytes=64)
+            nc.vector.quantize_mx(
+                out=x_codes[:].rearrange("q g t -> q (g t)").bitcast(FP8X4),
+                scales=x_scales[:].rearrange("q g t -> q (g t)"),
+                in_=grouped_of[c][:].rearrange("q g t j -> q (g t j)"),
+            )
+            quantised_of[c] = (x_codes, x_scales)
 
-        def multiply_sets(c, sets):
-            tokens = slice(P * sets[0], P * (sets[-1] + 1))
-            for b in range(F_BLOCKS):
-                vt = psum_vt.tile([P, P * len(sets)], F32, name="vt")
+        def multiply_chunk(c, h):
+            x_codes, x_scales = quantised_of[c]
+            for b in range((BANK // P) * h, (BANK // P) * (h + 1)):
+                vt = psum_vt.tile([P, CHUNK_TOKENS], F32, name="vt")
                 for g in range(K_GROUPS):
                     nc.tensor.matmul_mx(
                         out=vt[:],
                         lhsT=w_words[:, g, 2 * P * b : 2 * P * (b + 1)].bitcast(FP4X4),
                         lhsT_scale=w_scales[:, g, P * b : P * (b + 1)],
-                        rhs=codes_of[c][:, g, tokens].bitcast(FP8X4),
-                        rhs_scale=scales_of[c][:, g, tokens],
+                        rhs=x_codes[:, g, :].bitcast(FP8X4),
+                        rhs_scale=x_scales[:, g, :],
                         start=(g == 0),
                         stop=(g == K_GROUPS - 1),
                     )
-                nc.scalar.activation(
-                    out=vbT[c][:, b, tokens], in_=vt[:], func=ACT.Identity, bias=bias_col[:, b : b + 1], scale=1.0
-                )
+                nc.scalar.activation(out=vbT[c][:, b, :], in_=vt[:], func=ACT.Identity, bias=bias_col[:, b : b + 1], scale=1.0)
 
-        def transpose_back(r):
+        def add_taps(r, h):
             c = (r % SETS) // CHUNK_SETS
             first = ((r % SETS) % CHUNK_SETS) * P + r // SETS
-            rows_of[r] = []
-            for h in range(HALVES):
-                vp = psum_vp.tile([P, BANK], F32, name="vp")
-                for q in range(BANK // P):
-                    nc.tensor.transpose(
-                        vp[:, P * q : P * (q + 1)], vbT[c][:, (BANK // P) * h + q, first : first + P], ident[:]
-                    )
-                rows_of[r].append(vp)
-
-        def add_taps(r):
-            dests = range(max(r - NB, 0), min(r + NB, SETS - 1) + 1)
-            for h in range(HALVES):
-                cols = slice(BANK * h, BANK * (h + 1))
-                for d in dests:
-                    j = r - d + NB
-                    nc.vector.scalar_tensor_tensor(
-                        out=acc[d][:, cols],
-                        in0=rows_of[r][h][:],
-                        scalar=band[:, TAPS * d + j : TAPS * d + j + 1],
-                        in1=x_sb[d][:, cols] if taps_added[d] == 0 else acc[d][:, cols],
-                        op0=ALU.mult,
-                        op1=ALU.add,
-                        accum_out=row_sums[d][:, h : h + 1] if taps_added[d] == TAPS - 1 else None,
-                    )
-            for d in dests:
-                taps_added[d] += 1
-            return [d for d in dests if taps_added[d] == TAPS]
+            vp = psum_vp.tile([P, BANK], F32, name="vp")
+            for q in range(BANK // P):
+                nc.tensor.transpose(
+                    vp[:, P * q : P * (q + 1)], vbT[c][:, (BANK // P) * h + q, first : first + P], ident[:]
+                )
+            cols = slice(BANK * h, BANK * (h + 1))
+            for d in range(max(r - NB, 0), min(r + NB, SETS - 1) + 1):
+                j = r - d + NB
+                nc.vector.scalar_tensor_tensor(
+                    out=acc[d][:, cols],
+                    in0=vp[:],
+                    scalar=band[:, TAPS * d + j : TAPS * d + j + 1],
+                    in1=x_sb[d][:, cols] if taps_added[h][d] == 0 else acc[d][:, cols],
+                    op0=ALU.mult,
+                    op1=ALU.add,
+                    accum_out=row_sums[d][:, h : h + 1] if taps_added[h][d] == TAPS - 1 else None,
+                )
+                taps_added[h][d] += 1
 
         def normalise_set(d):
             halves = stats.tile([P, HALVES], F32, name="halves")
@@ -207,14 +188,20 @@ def tile_crosssliceattention_pb_kernel(tc, x, Wv_words, Wv_scales, bv, attn_band
                 )
             nc.sync.dma_start(out=out_by_set[:, d, :], in_=acc[d][:])
 
-        begin_chunk(chunk_order[0])
-        for i in range(CHUNK_SETS):
-            project_sets(chunk_order[0], [i])
-        for c in chunk_order[1:]:
-            begin_chunk(c)
-            project_sets(c, list(range(CHUNK_SETS)))
-        for r in set_order:
-            with tc.high_priority():
-                transpose_back(r)
-            for d in add_taps(r):
-                normalise_set(d)
+        transpose_chunk(chunk_order[0])
+        quantise_chunk(chunk_order[0])
+        normalised = 0
+        for pair in range(len(set_order) // 2):
+            for h in range(HALVES):
+                if pair == 0:
+                    multiply_chunk(chunk_order[0], h)
+                for r in set_order[2 * pair : 2 * pair + 2]:
+                    add_taps(r, h)
+            if pair + 1 < CHUNKS:
+                transpose_chunk(chunk_order[pair + 1])
+                quantise_chunk(chunk_order[pair + 1])
+                for h in range(HALVES):
+                    multiply_chunk(chunk_order[pair + 1], h)
+            while normalised < SETS and taps_added[HALVES - 1][normalised] == TAPS:
+                normalise_set(normalised)
+                normalised += 1

@@ -12,40 +12,50 @@ FP8X4 = mybir.dt.float8_e4m3fn_x4
 FP4X4 = mybir.dt.float4_e2m1fn_x4
 ACT = mybir.ActivationFunctionType
 ALU = mybir.AluOpType
+AXIS = mybir.AxisListType
 
 P = 128
 D = 1024
 TOKENS = 4 * 512
-SETS = TOKENS // P
-CHUNK_SETS = 4
-CHUNKS = SETS // CHUNK_SETS
-CHUNK_TOKENS = CHUNK_SETS * P
 K_GROUPS = D // 512
-F_BLOCKS = D // P
 BANK = 512
 HALVES = D // BANK
 NB = 2
 TAPS = 2 * NB + 1
 LN_EPS = 1e-5
 
+V_SETS = 5
+V_TOKENS = V_SETS * P
+PE_TILES = 12
+PE_STEP = 120
+PE_FIRST = TOKENS - PE_TILES * PE_STEP
+BIAS_ROW = P - 1
+V_BUFS = 3
+Z_WIDTH = P + 2 * NB
+Z_ROW = (PE_TILES + 1) * Z_WIDTH
+
 FLOPS = 2 * TOKENS * D * D
+
+GPSIMD_SETS = (0, 1, 2, 3, 4)
+GPSIMD_TILES = (0, 2, 4, 6, 8)
 
 
 def tile_crosssliceattention_pb_kernel(tc, x, Wv_words, Wv_scales, bv, attn_band, gamma, beta, out):
     nc = tc.nc
-    x_by_set = x.flatten_outer_dims().rearrange("(p r) d -> p r d", r=SETS)
-    out_by_set = out.flatten_outer_dims().rearrange("(p r) d -> p r d", r=SETS)
-
-    chunk_order = [0, CHUNKS - 1] + list(range(1, CHUNKS - 1))
-    set_order = list(range(CHUNK_SETS)) + list(range(-NB, 0)) + list(range(CHUNK_SETS, SETS + NB))
+    x_rows = x.flatten_outer_dims()
+    out_rows = out.flatten_outer_dims()
+    band_rows = attn_band.flatten_outer_dims()
+    out_flat = out_rows.rearrange("s d -> (s d)")
+    scratch_base = (TOKENS - (P * Z_ROW + D - 1) // D) * D
 
     with ExitStack() as ctx:
         keep = ctx.enter_context(tc.tile_pool(name="keep", bufs=1))
-        stage = ctx.enter_context(tc.tile_pool(name="stage", bufs=2))
+        stage = ctx.enter_context(tc.tile_pool(name="stage", bufs=3))
         stats = ctx.enter_context(tc.tile_pool(name="stats", bufs=4))
         psum_xt = ctx.enter_context(tc.psum_pool(name="psum_xt", bufs=2))
-        psum_vt = ctx.enter_context(tc.psum_pool(name="psum_vt", bufs=2))
-        psum_vp = ctx.enter_context(tc.psum_pool(name="psum_vp", bufs=2 * HALVES))
+        psum_vv = ctx.enter_context(tc.psum_pool(name="psum_vv", bufs=2))
+        psum_vw = ctx.enter_context(tc.psum_pool(name="psum_vw", bufs=2))
+        psum_mix = ctx.enter_context(tc.psum_pool(name="psum_mix", bufs=2))
 
         ident = keep.tile([P, P], F32, name="ident")
         masks.make_identity(nc, ident[:])
@@ -55,18 +65,44 @@ def tile_crosssliceattention_pb_kernel(tc, x, Wv_words, Wv_scales, bv, attn_band
         nc.scalar.activation(out=warm[:], in_=eps_col[:], func=ACT.Abs_reciprocal_sqrt)
         w_scales = keep.tile([P, K_GROUPS, D], U8, name="w_scales", align_bytes=64)
         nc.vector.memset(w_scales[:].rearrange("p g n -> p (g n)").bitcast(I32), 0)
-        bias_rows = keep.tile([P, P], F32, name="bias_rows")
-        nc.vector.memset(bias_rows[:], 0.0)
+        band_w_bf = keep.tile([P, PE_TILES, TAPS], BF16, name="band_w_bf")
+        nc.vector.memset(band_w_bf[:], 0.0)
+        z_rows = keep.tile([P, PE_TILES + 1, Z_WIDTH], F32, name="z_rows")
+        nc.vector.memset(z_rows[:], 0.0)
 
-        x_sb = [keep.tile([P, D], BF16, name="x_sb%d" % r) for r in range(SETS)]
+        x_set = {}
+        for r in range(-NB, V_SETS + NB):
+            x_set[r] = keep.tile([P, D], BF16, name="x_set%d" % (r + NB))
+        x_win = [keep.tile([P, D], BF16, name="x_win%d" % t) for t in range(PE_TILES)]
+        for r in range(-NB, 0):
+            nc.gpsimd.memset(x_set[r][0:1, :], 0.0)
+        nc.gpsimd.memset(x_win[PE_TILES - 1][:], 0.0)
 
-        def load_chunk(c):
-            for r in range(CHUNK_SETS * c, CHUNK_SETS * (c + 1)):
-                nc.sync.dma_start(out=x_sb[r][:], in_=x_by_set[:, r, :])
+        def load_set(r):
+            if r < 0:
+                src = x_rows[0 : V_TOKENS - V_SETS].rearrange("(p r) d -> p r d", r=V_SETS)[:, r + V_SETS, :]
+                nc.sync.dma_start(out=x_set[r][1:113, :], in_=src[0:112, :])
+                nc.sync.dma_start(out=x_set[r][113:P, :], in_=src[112 : P - 1, :])
+            elif r < V_SETS:
+                nc.sync.dma_start(out=x_set[r][:], in_=x_rows[0:V_TOKENS].rearrange("(p r) d -> p r d", r=V_SETS)[:, r, :])
+            else:
+                src = x_rows[V_SETS : V_TOKENS + V_SETS].rearrange("(p r) d -> p r d", r=V_SETS)[:, r - V_SETS, :]
+                nc.sync.dma_start(out=x_set[r][:], in_=src)
 
-        bias_bf = keep.tile([F_BLOCKS, P], BF16, name="bias_bf")
-        nc.sync.dma_start(out=bias_bf[:], in_=bv.rearrange("(b f) -> b f", f=P))
-        load_chunk(chunk_order[0])
+        def load_window(t):
+            first = PE_FIRST - NB + PE_STEP * t
+            rows = min(P, TOKENS - first)
+            whole = rows - rows % 16
+            nc.sync.dma_start(out=x_win[t][0:whole, :], in_=x_rows[first : first + whole, :])
+            if whole < rows:
+                nc.sync.dma_start(out=x_win[t][whole:rows, :], in_=x_rows[first + whole : first + rows, :])
+
+        band_v_bf = keep.tile([P, V_SETS, TAPS], BF16, name="band_v_bf")
+        nc.sync.dma_start(out=band_v_bf[:], in_=band_rows[0:V_TOKENS].rearrange("(p r) j -> p r j", r=V_SETS))
+        nc.sync.dma_start(
+            out=band_w_bf[NB : NB + PE_STEP, :, :], in_=band_rows[PE_FIRST:TOKENS].rearrange("(t m) j -> m t j", m=PE_STEP)
+        )
+        load_set(0)
         for quad in range(4):
             nc.sync.dma_start(
                 out=w_scales[32 * quad : 32 * quad + 4, :, :].bitcast(I32),
@@ -74,134 +110,194 @@ def tile_crosssliceattention_pb_kernel(tc, x, Wv_words, Wv_scales, bv, attn_band
             )
         w_words = keep.tile([P, K_GROUPS, 2 * D], U8, name="w_words", align_bytes=64)
         nc.sync.dma_start(out=w_words[:].bitcast(I32), in_=Wv_words.rearrange("g p n -> p g n").bitcast(I32))
-        band_bf = keep.tile([P, SETS * TAPS], BF16, name="band_bf")
-        nc.sync.dma_start(out=band_bf[:], in_=attn_band.flatten_outer_dims().rearrange("(p r) j -> p (r j)", r=SETS))
-        for c in chunk_order[1:]:
-            load_chunk(c)
+        bias_bf = keep.tile([P, D], BF16, name="bias_bf")
+        nc.sync.dma_start(out=bias_bf[:], in_=bv.partition_broadcast(P))
+
+        nc.vector.tensor_copy(out=z_rows[:, 0:PE_TILES, 0:TAPS], in_=band_w_bf[:])
+        a_sum_w = keep.tile([P, PE_TILES], F32, name="a_sum_w")
+        nc.vector.tensor_reduce(out=a_sum_w[:], in_=z_rows[:, 0:PE_TILES, 0:TAPS], axis=AXIS.X, op=ALU.add)
+        nc.sync.dma_start(
+            out=out_flat[scratch_base : scratch_base + P * Z_ROW].rearrange("(m w) -> m w", w=Z_ROW),
+            in_=z_rows[:].rearrange("m t c -> m (t c)"),
+        )
+        for r in (1, 2, -2, -1):
+            load_set(r)
+        a_tok = keep.tile([P, PE_TILES, P], F32, name="a_tok")
+        skewed = out_flat[scratch_base + NB : scratch_base + NB + P * (Z_ROW - 1)].rearrange("(m w) -> m w", w=Z_ROW - 1)
+        nc.sync.dma_start(
+            out=a_tok[:], in_=skewed[:, 0 : PE_TILES * Z_WIDTH].rearrange("m (t c) -> m t c", c=Z_WIDTH)[:, :, 0:P]
+        )
+        for r in (3, 4, 5, 6):
+            load_set(r)
+        load_window(0)
+        load_window(1)
         gamma_bf = keep.tile([P, D], BF16, name="gamma_bf")
         nc.sync.dma_start(out=gamma_bf[:], in_=gamma.partition_broadcast(P))
         beta_bf = keep.tile([P, D], BF16, name="beta_bf")
         nc.sync.dma_start(out=beta_bf[:], in_=beta.partition_broadcast(P))
+        for t in range(2, PE_TILES):
+            load_window(t)
 
-        nc.vector.tensor_copy(out=bias_rows[0:F_BLOCKS, :], in_=bias_bf[:])
-        bias_ps = psum_xt.tile([P, P], F32, name="bias_ps", tag="xt")
-        nc.tensor.transpose(bias_ps[:], bias_rows[:], ident[:])
-        bias_col = keep.tile([P, F_BLOCKS], F32, name="bias_col")
-        nc.vector.tensor_copy(out=bias_col[:], in_=bias_ps[:, 0:F_BLOCKS])
-        band = keep.tile([P, SETS * TAPS], F32, name="band")
-        nc.vector.tensor_copy(out=band[:], in_=band_bf[:])
-        gamma_f = keep.tile([P, D], F32, name="gamma_f")
-        nc.gpsimd.tensor_scalar(out=gamma_f[:], in0=gamma_bf[:], scalar1=1.0, scalar2=0.0, op0=ALU.mult, op1=ALU.add)
-        beta_f = keep.tile([P, D], F32, name="beta_f")
-        nc.gpsimd.tensor_scalar(out=beta_f[:], in0=beta_bf[:], scalar1=1.0, scalar2=0.0, op0=ALU.mult, op1=ALU.add)
+        band_v = keep.tile([P, V_SETS, TAPS], F32, name="band_v")
+        nc.vector.tensor_copy(out=band_v[:], in_=band_v_bf[:])
+        a_sum_v = keep.tile([P, V_SETS], F32, name="a_sum_v")
+        nc.vector.tensor_reduce(out=a_sum_v[:], in_=band_v[:], axis=AXIS.X, op=ALU.add)
+        nc.vector.tensor_copy(out=a_tok[:, :, BIAS_ROW : BIAS_ROW + 1], in_=a_sum_w[:].unsqueeze(2))
+        v_sb = [keep.tile([P, D], F32, name="v_sb%d" % i) for i in range(V_BUFS)]
+        for i in range(V_BUFS):
+            nc.gpsimd.tensor_copy(out=v_sb[i][96:P, :], in_=bias_bf[96:P, :])
 
-        vbT = [keep.tile([P, F_BLOCKS, CHUNK_TOKENS], F32, name="vbT%d" % c) for c in range(CHUNKS)]
-        acc = [keep.tile([P, D], F32, name="acc%d" % d) for d in range(SETS)]
-        row_sums = [keep.tile([P, HALVES], F32, name="row_sums%d" % d) for d in range(SETS)]
-        taps_added = [[0] * SETS for h in range(HALVES)]
+        acc = [keep.tile([P, D], F32, name="acc%d" % d) for d in range(V_SETS)]
+        o_win = [keep.tile([P, D], F32, name="o_win%d" % t) for t in range(PE_TILES)]
+        sums_v = [keep.tile([P, HALVES], F32, name="sums_v%d" % d) for d in range(V_SETS)]
+        sums_w = [keep.tile([P, HALVES], F32, name="sums_w%d" % t) for t in range(PE_TILES)]
+        a_T = keep.tile([P, PE_TILES, P], F32, name="a_T")
+        taps_added = [[0] * V_SETS for h in range(HALVES)]
         grouped_of = {}
         quantised_of = {}
+        v_of = {}
 
-        def transpose_chunk(c):
-            grouped = stage.tile([P, K_GROUPS, CHUNK_TOKENS, 4], BF16, name="grouped", align_bytes=64)
-            grouped_words = grouped[:].bitcast(F32)
-            for i in range(CHUNK_SETS):
-                x_words = x_sb[CHUNK_SETS * c + i][:].bitcast(F32)
-                xt = psum_xt.tile([P, K_GROUPS, 2, P], F32, name="xt", tag="xt")
-                for g in range(K_GROUPS):
-                    for u in range(2):
-                        nc.tensor.transpose(xt[:, g, u, :], x_words[:, 256 * g + u : 256 * (g + 1) : 2], ident[:])
-                nc.scalar.copy(
-                    out=grouped_words[:, :, P * i : P * (i + 1), :], in_=xt[:].rearrange("q g u t -> q g t u")
+        def start_sums():
+            for d in range(V_SETS):
+                nc.vector.scalar_tensor_tensor(
+                    out=acc[d][:], in0=bias_bf[:], scalar=a_sum_v[:, d : d + 1], in1=x_set[d][:], op0=ALU.mult, op1=ALU.add
                 )
-            grouped_of[c] = grouped
 
-        def quantise_chunk(c):
-            x_codes = stage.tile([P, K_GROUPS, CHUNK_TOKENS], U32, name="x_codes", align_bytes=64)
-            x_scales = stage.tile([P, K_GROUPS, CHUNK_TOKENS], U8, name="x_scales", align_bytes=64)
+        def transpose_bands():
+            for q in range(PE_TILES // 4):
+                at_ps = psum_xt.tile([P, 4, P], F32, name="at_ps", tag="xt")
+                for i in range(4):
+                    nc.tensor.transpose(at_ps[:, i, :], a_tok[:, 4 * q + i, :], ident[:])
+                nc.scalar.copy(out=a_T[:, 4 * q : 4 * q + 4, :], in_=at_ps[:])
+
+        def x_of(unit):
+            return x_set[unit[1]] if unit[0] == "set" else x_win[unit[1]]
+
+        def transpose_unit(unit):
+            grouped = stage.tile([P, K_GROUPS, P, 4], BF16, name="grouped", align_bytes=64)
+            x_words = x_of(unit)[:].bitcast(F32)
+            xt = psum_xt.tile([P, K_GROUPS, 2, P], F32, name="xt", tag="xt")
+            for g in range(K_GROUPS):
+                for u in range(2):
+                    nc.tensor.transpose(xt[:, g, u, :], x_words[:, 256 * g + u : 256 * (g + 1) : 2], ident[:])
+            nc.scalar.copy(out=grouped[:].bitcast(F32), in_=xt[:].rearrange("q g u t -> q g t u"))
+            grouped_of[unit] = grouped
+
+        def quantise_unit(unit):
+            x_codes = stage.tile([P, K_GROUPS, P], U32, name="x_codes", align_bytes=64)
+            x_scales = stage.tile([P, K_GROUPS, P], U8, name="x_scales", align_bytes=64)
             nc.vector.quantize_mx(
                 out=x_codes[:].rearrange("q g t -> q (g t)").bitcast(FP8X4),
                 scales=x_scales[:].rearrange("q g t -> q (g t)"),
-                in_=grouped_of[c][:].rearrange("q g t j -> q (g t j)"),
+                in_=grouped_of[unit][:].rearrange("q g t j -> q (g t j)"),
             )
-            quantised_of[c] = (x_codes, x_scales)
+            quantised_of[unit] = (x_codes, x_scales)
 
-        def multiply_chunk(c, h):
-            x_codes, x_scales = quantised_of[c]
-            for b in range((BANK // P) * h, (BANK // P) * (h + 1)):
-                vt = psum_vt.tile([P, CHUNK_TOKENS], F32, name="vt")
+        def project_unit(unit):
+            x_codes, x_scales = quantised_of[unit]
+            pool = psum_vv if unit[0] == "set" else psum_vw
+            banks = []
+            for h in range(HALVES):
+                v_ps = pool.tile([P, BANK], F32, name="v_ps")
                 for g in range(K_GROUPS):
                     nc.tensor.matmul_mx(
-                        out=vt[:],
-                        lhsT=w_words[:, g, 2 * P * b : 2 * P * (b + 1)].bitcast(FP4X4),
-                        lhsT_scale=w_scales[:, g, P * b : P * (b + 1)],
-                        rhs=x_codes[:, g, :].bitcast(FP8X4),
-                        rhs_scale=x_scales[:, g, :],
+                        out=v_ps[:],
+                        lhsT=x_codes[:, g, :].bitcast(FP8X4),
+                        lhsT_scale=x_scales[:, g, :],
+                        rhs=w_words[:, g, 2 * BANK * h : 2 * BANK * (h + 1)].bitcast(FP4X4),
+                        rhs_scale=w_scales[:, g, BANK * h : BANK * (h + 1)],
                         start=(g == 0),
                         stop=(g == K_GROUPS - 1),
                     )
-                nc.scalar.activation(out=vbT[c][:, b, :], in_=vt[:], func=ACT.Identity, bias=bias_col[:, b : b + 1], scale=1.0)
+                banks.append(v_ps)
+                if unit[0] == "win":
+                    nc.scalar.copy(out=v_sb[unit[1] % V_BUFS][0:BIAS_ROW, BANK * h : BANK * (h + 1)], in_=v_ps[0:BIAS_ROW, :])
+            v_of[unit] = banks
 
-        def add_taps(r, h):
-            c = (r % SETS) // CHUNK_SETS
-            first = ((r % SETS) % CHUNK_SETS) * P + r // SETS
-            vp = psum_vp.tile([P, BANK], F32, name="vp")
-            for q in range(BANK // P):
-                nc.tensor.transpose(
-                    vp[:, P * q : P * (q + 1)], vbT[c][:, (BANK // P) * h + q, first : first + P], ident[:]
-                )
-            cols = slice(BANK * h, BANK * (h + 1))
-            for d in range(max(r - NB, 0), min(r + NB, SETS - 1) + 1):
-                j = r - d + NB
+        def add_taps(r):
+            for h in range(HALVES):
+                cols = slice(BANK * h, BANK * (h + 1))
+                for d in range(max(r - NB, 0), min(r + NB, V_SETS - 1) + 1):
+                    j = r - d + NB
+                    nc.vector.scalar_tensor_tensor(
+                        out=acc[d][:, cols],
+                        in0=v_of[("set", r)][h][:],
+                        scalar=band_v[:, d, j : j + 1],
+                        in1=acc[d][:, cols],
+                        op0=ALU.mult,
+                        op1=ALU.add,
+                        accum_out=sums_v[d][:, h : h + 1] if taps_added[h][d] == TAPS - 1 else None,
+                    )
+                    taps_added[h][d] += 1
+
+        def mix_window(t):
+            for h in range(HALVES):
+                cols = slice(BANK * h, BANK * (h + 1))
+                mix_ps = psum_mix.tile([P, BANK], F32, name="mix_ps")
+                nc.tensor.matmul(out=mix_ps[:], lhsT=a_T[:, t, :], rhs=v_sb[t % V_BUFS][:, cols], start=True, stop=True)
                 nc.vector.scalar_tensor_tensor(
-                    out=acc[d][:, cols],
-                    in0=vp[:],
-                    scalar=band[:, TAPS * d + j : TAPS * d + j + 1],
-                    in1=x_sb[d][:, cols] if taps_added[h][d] == 0 else acc[d][:, cols],
+                    out=o_win[t][:, cols],
+                    in0=mix_ps[:],
+                    scalar=1.0,
+                    in1=x_win[t][:, cols],
                     op0=ALU.mult,
                     op1=ALU.add,
-                    accum_out=row_sums[d][:, h : h + 1] if taps_added[h][d] == TAPS - 1 else None,
+                    accum_out=sums_w[t][:, h : h + 1],
                 )
-                taps_added[h][d] += 1
 
-        def normalise_set(d):
+        def normalise(o, row_sums, on_gpsimd):
             halves = stats.tile([P, HALVES], F32, name="halves")
             neg_mean = stats.tile([P, 1], F32, name="neg_mean")
-            nc.scalar.activation(out=halves[:], in_=row_sums[d][:], func=ACT.Identity, scale=-1.0 / D, accum_out=neg_mean[:])
+            nc.scalar.activation(out=halves[:], in_=row_sums[:], func=ACT.Identity, scale=-1.0 / D, accum_out=neg_mean[:])
             squares = stage.tile([P, D], BF16, name="squares")
             sum_sq = stats.tile([P, 1], F32, name="sum_sq")
-            nc.scalar.activation(out=squares[:], in_=acc[d][:], func=ACT.Square, bias=neg_mean[:], scale=1.0, accum_out=sum_sq[:])
+            nc.scalar.activation(out=squares[:], in_=o[:], func=ACT.Square, bias=neg_mean[:], scale=1.0, accum_out=sum_sq[:])
             rstd = stats.tile([P, 1], F32, name="rstd")
             nc.scalar.activation(out=rstd[:], in_=sum_sq[:], func=ACT.Abs_reciprocal_sqrt, bias=eps_col[:], scale=1.0 / D)
-            if d < SETS - NB:
+            if on_gpsimd:
                 shift = stats.tile([P, 1], F32, name="shift")
                 nc.scalar.activation(out=shift[:], in_=neg_mean[:], func=ACT.Copy, scale=rstd[:])
-                nc.scalar.activation(out=acc[d][:], in_=acc[d][:], func=ACT.Identity, bias=shift[:], scale=rstd[:])
-                nc.gpsimd.tensor_tensor(out=acc[d][:], in0=acc[d][:], in1=gamma_f[:], op=ALU.mult)
-                nc.gpsimd.tensor_tensor(out=acc[d][:], in0=acc[d][:], in1=beta_f[:], op=ALU.add)
+                nc.scalar.activation(out=o[:], in_=o[:], func=ACT.Identity, bias=shift[:], scale=rstd[:])
+                nc.gpsimd.tensor_tensor(out=o[:], in0=o[:], in1=gamma_bf[:], op=ALU.mult)
+                nc.gpsimd.tensor_tensor(out=o[:], in0=o[:], in1=beta_bf[:], op=ALU.add)
             else:
-                nc.vector.scalar_tensor_tensor(
-                    out=acc[d][:], in0=acc[d][:], scalar=neg_mean[:], in1=gamma_f[:], op0=ALU.add, op1=ALU.mult
-                )
-                nc.vector.scalar_tensor_tensor(
-                    out=acc[d][:], in0=acc[d][:], scalar=rstd[:], in1=beta_f[:], op0=ALU.mult, op1=ALU.add
-                )
-            nc.sync.dma_start(out=out_by_set[:, d, :], in_=acc[d][:])
+                nc.vector.scalar_tensor_tensor(out=o[:], in0=o[:], scalar=neg_mean[:], in1=gamma_bf[:], op0=ALU.add, op1=ALU.mult)
+                nc.vector.scalar_tensor_tensor(out=o[:], in0=o[:], scalar=rstd[:], in1=beta_bf[:], op0=ALU.mult, op1=ALU.add)
 
-        transpose_chunk(chunk_order[0])
-        quantise_chunk(chunk_order[0])
-        normalised = 0
-        for pair in range(len(set_order) // 2):
-            for h in range(HALVES):
-                if pair == 0:
-                    multiply_chunk(chunk_order[0], h)
-                for r in set_order[2 * pair : 2 * pair + 2]:
-                    add_taps(r, h)
-            if pair + 1 < CHUNKS:
-                transpose_chunk(chunk_order[pair + 1])
-                quantise_chunk(chunk_order[pair + 1])
-                for h in range(HALVES):
-                    multiply_chunk(chunk_order[pair + 1], h)
-            while normalised < SETS and taps_added[HALVES - 1][normalised] == TAPS:
-                normalise_set(normalised)
-                normalised += 1
+        def finish_unit(unit):
+            if unit[0] == "set":
+                add_taps(unit[1])
+                for d in range(V_SETS):
+                    if taps_added[HALVES - 1][d] == TAPS:
+                        taps_added[HALVES - 1][d] += 1
+                        normalise(acc[d], sums_v[d], d in GPSIMD_SETS)
+                        nc.sync.dma_start(
+                            out=out_rows[0:V_TOKENS].rearrange("(p r) d -> p r d", r=V_SETS)[:, d, :], in_=acc[d][:]
+                        )
+            else:
+                t = unit[1]
+                mix_window(t)
+                normalise(o_win[t], sums_w[t], t in GPSIMD_TILES)
+                first = max(PE_FIRST + PE_STEP * t, V_TOKENS)
+                last = PE_FIRST + PE_STEP * (t + 1)
+                row = first - (PE_FIRST - NB + PE_STEP * t)
+                nc.sync.dma_start(out=out_rows[first:last, :], in_=o_win[t][row : row + last - first, :])
+
+        order = [("set", r) for r in (0, 1, 2, -2, -1)]
+        later_sets = [3, 4, 5, 6]
+        for t in range(PE_TILES):
+            order.append(("win", t))
+            if t % 2 == 1 and later_sets:
+                order.append(("set", later_sets.pop(0)))
+
+        start_sums()
+        for i in range(len(order) + 2):
+            if i < len(order):
+                transpose_unit(order[i])
+            if i == 3:
+                transpose_bands()
+            if 1 <= i <= len(order):
+                quantise_unit(order[i - 1])
+                project_unit(order[i - 1])
+            if i >= 2:
+                finish_unit(order[i - 2])

@@ -20,6 +20,7 @@ TOKENS = 4 * 512
 K_GROUPS = D // 512
 BANK = 512
 HALVES = D // BANK
+F_BLOCKS = D // P
 NB = 2
 TAPS = 2 * NB + 1
 LN_EPS = 1e-5
@@ -52,13 +53,16 @@ def tile_crosssliceattention_pb_kernel(tc, x, Wv_words, Wv_scales, bv, attn_band
         keep = ctx.enter_context(tc.tile_pool(name="keep", bufs=1))
         stage = ctx.enter_context(tc.tile_pool(name="stage", bufs=3))
         stats = ctx.enter_context(tc.tile_pool(name="stats", bufs=4))
-        psum_xt = ctx.enter_context(tc.psum_pool(name="psum_xt", bufs=2))
         psum_vv = ctx.enter_context(tc.psum_pool(name="psum_vv", bufs=2))
         psum_vw = ctx.enter_context(tc.psum_pool(name="psum_vw", bufs=2))
         psum_mix = ctx.enter_context(tc.psum_pool(name="psum_mix", bufs=2))
 
         ident = keep.tile([P, P], F32, name="ident")
         masks.make_identity(nc, ident[:])
+        ident_bf = keep.tile([P, P], BF16, name="ident_bf")
+        masks.make_identity(nc, ident_bf[:])
+        gb_rows = keep.tile([P, P], BF16, name="gb_rows")
+        nc.vector.memset(gb_rows[:], 0.0)
         eps_col = keep.tile([P, 1], F32, name="eps_col")
         nc.vector.memset(eps_col[:], LN_EPS)
         warm = keep.tile([P, 1], F32, name="warm")
@@ -127,6 +131,8 @@ def tile_crosssliceattention_pb_kernel(tc, x, Wv_words, Wv_scales, bv, attn_band
         nc.sync.dma_start(
             out=a_tok[:], in_=skewed[:, 0 : PE_TILES * Z_WIDTH].rearrange("m (t c) -> m t c", c=Z_WIDTH)[:, :, 0:P]
         )
+        nc.sync.dma_start(out=gb_rows[0:F_BLOCKS, :], in_=gamma.rearrange("(b f) -> b f", f=P))
+        nc.sync.dma_start(out=gb_rows[F_BLOCKS : 2 * F_BLOCKS, :], in_=beta.rearrange("(b f) -> b f", f=P))
         for r in (3, 4, 5, 6):
             load_set(r)
         load_window(0)
@@ -153,6 +159,7 @@ def tile_crosssliceattention_pb_kernel(tc, x, Wv_words, Wv_scales, bv, attn_band
         sums_w = [keep.tile([P, HALVES], F32, name="sums_w%d" % t) for t in range(PE_TILES)]
         a_T = keep.tile([P, PE_TILES, P], F32, name="a_T")
         taps_added = [[0] * V_SETS for h in range(HALVES)]
+        spread = []
         grouped_of = {}
         quantised_of = {}
         v_of = {}
@@ -163,7 +170,14 @@ def tile_crosssliceattention_pb_kernel(tc, x, Wv_words, Wv_scales, bv, attn_band
                     out=acc[d][:], in0=bias_bf[:], scalar=a_sum_v[:, d : d + 1], in1=x_set[d][:], op0=ALU.mult, op1=ALU.add
                 )
 
-        def transpose_bands():
+        gb_col = keep.tile([P, 2 * F_BLOCKS], BF16, name="gb_col")
+
+        def transpose_gain_and_shift(psum_xt):
+            gb_ps = psum_xt.tile([P, P], BF16, name="gb_ps", tag="xt")
+            nc.tensor.transpose(gb_ps[:], gb_rows[:], ident_bf[:])
+            nc.vector.tensor_copy(out=gb_col[:], in_=gb_ps[:, 0 : 2 * F_BLOCKS])
+
+        def transpose_bands(psum_xt):
             for q in range(PE_TILES // 4):
                 at_ps = psum_xt.tile([P, 4, P], F32, name="at_ps", tag="xt")
                 for i in range(4):
@@ -173,25 +187,27 @@ def tile_crosssliceattention_pb_kernel(tc, x, Wv_words, Wv_scales, bv, attn_band
         def x_of(unit):
             return x_set[unit[1]] if unit[0] == "set" else x_win[unit[1]]
 
-        def transpose_unit(unit):
-            grouped = stage.tile([P, K_GROUPS, P, 4], BF16, name="grouped", align_bytes=64)
-            x_words = x_of(unit)[:].bitcast(F32)
-            xt = psum_xt.tile([P, K_GROUPS, 2, P], F32, name="xt", tag="xt")
-            for g in range(K_GROUPS):
-                for u in range(2):
-                    nc.tensor.transpose(xt[:, g, u, :], x_words[:, 256 * g + u : 256 * (g + 1) : 2], ident[:])
-            nc.scalar.copy(out=grouped[:].bitcast(F32), in_=xt[:].rearrange("q g u t -> q g t u"))
-            grouped_of[unit] = grouped
+        def transpose_units(psum_xt, n, units):
+            grouped = stage.tile([P, len(units), K_GROUPS, P, 4], BF16, name="grouped", align_bytes=64)
+            for i, unit in enumerate(units):
+                x_words = x_of(unit)[:].bitcast(F32)
+                xt = psum_xt.tile([P, K_GROUPS, 2, P], F32, name="xt", tag="xt")
+                for g in range(K_GROUPS):
+                    for u in range(2):
+                        nc.tensor.transpose(xt[:, g, u, :], x_words[:, 256 * g + u : 256 * (g + 1) : 2], ident[:])
+                nc.scalar.copy(out=grouped[:, i].bitcast(F32), in_=xt[:].rearrange("q g u t -> q g t u"))
+            grouped_of[n] = grouped
 
-        def quantise_unit(unit):
-            x_codes = stage.tile([P, K_GROUPS, P], U32, name="x_codes", align_bytes=64)
-            x_scales = stage.tile([P, K_GROUPS, P], U8, name="x_scales", align_bytes=64)
+        def quantise_units(n, units):
+            x_codes = keep.tile([P, len(units), K_GROUPS, P], U32, name="x_codes%d" % n, align_bytes=64)
+            x_scales = keep.tile([P, len(units), K_GROUPS, P], U8, name="x_scales%d" % n, align_bytes=64)
             nc.vector.quantize_mx(
-                out=x_codes[:].rearrange("q g t -> q (g t)").bitcast(FP8X4),
-                scales=x_scales[:].rearrange("q g t -> q (g t)"),
-                in_=grouped_of[unit][:].rearrange("q g t j -> q (g t j)"),
+                out=x_codes[:].rearrange("q i g t -> q (i g t)").bitcast(FP8X4),
+                scales=x_scales[:].rearrange("q i g t -> q (i g t)"),
+                in_=grouped_of[n][:].rearrange("q i g t j -> q (i g t j)"),
             )
-            quantised_of[unit] = (x_codes, x_scales)
+            for i, unit in enumerate(units):
+                quantised_of[unit] = (x_codes[:, i], x_scales[:, i])
 
         def project_unit(unit):
             x_codes, x_scales = quantised_of[unit]
@@ -261,8 +277,9 @@ def tile_crosssliceattention_pb_kernel(tc, x, Wv_words, Wv_scales, bv, attn_band
                 nc.gpsimd.tensor_tensor(out=o[:], in0=o[:], in1=gamma_bf[:], op=ALU.mult)
                 nc.gpsimd.tensor_tensor(out=o[:], in0=o[:], in1=beta_bf[:], op=ALU.add)
             else:
-                nc.vector.scalar_tensor_tensor(out=o[:], in0=o[:], scalar=neg_mean[:], in1=gamma_bf[:], op0=ALU.add, op1=ALU.mult)
-                nc.vector.scalar_tensor_tensor(out=o[:], in0=o[:], scalar=rstd[:], in1=beta_bf[:], op0=ALU.mult, op1=ALU.add)
+                gamma_ps, beta_ps = spread
+                nc.vector.scalar_tensor_tensor(out=o[:], in0=o[:], scalar=neg_mean[:], in1=gamma_ps[:], op0=ALU.add, op1=ALU.mult)
+                nc.vector.scalar_tensor_tensor(out=o[:], in0=o[:], scalar=rstd[:], in1=beta_ps[:], op0=ALU.mult, op1=ALU.add)
 
         def finish_unit(unit):
             if unit[0] == "set":
@@ -290,14 +307,28 @@ def tile_crosssliceattention_pb_kernel(tc, x, Wv_words, Wv_scales, bv, attn_band
             if t % 2 == 1 and later_sets:
                 order.append(("set", later_sets.pop(0)))
 
+        groups = [order[0:1]] + [order[i : i + 2] for i in range(1, len(order), 2)]
         start_sums()
-        for i in range(len(order) + 2):
+        with tc.psum_pool(name="psum_xt", bufs=2) as psum_xt:
+            for n in range(len(groups) + 1):
+                if n < len(groups):
+                    transpose_units(psum_xt, n, groups[n])
+                if n >= 1:
+                    quantise_units(n - 1, groups[n - 1])
+                if n == 3:
+                    transpose_bands(psum_xt)
+                    transpose_gain_and_shift(psum_xt)
+        psum_gb = ctx.enter_context(tc.psum_pool(name="psum_gb", bufs=1))
+        gamma_ps = psum_gb.tile([P, D], BF16, name="gamma_ps")
+        beta_ps = psum_gb.tile([P, D], BF16, name="beta_ps")
+        for b in range(F_BLOCKS):
+            nc.tensor.transpose(gamma_ps[:, P * b : P * (b + 1)], gb_col[:, b : b + 1].to_broadcast([P, P]), ident_bf[:])
+            nc.tensor.transpose(
+                beta_ps[:, P * b : P * (b + 1)], gb_col[:, F_BLOCKS + b : F_BLOCKS + b + 1].to_broadcast([P, P]), ident_bf[:]
+            )
+        spread.extend([gamma_ps, beta_ps])
+        for i in range(len(order) + 1):
             if i < len(order):
-                transpose_unit(order[i])
-            if i == 3:
-                transpose_bands()
-            if 1 <= i <= len(order):
-                quantise_unit(order[i - 1])
-                project_unit(order[i - 1])
-            if i >= 2:
-                finish_unit(order[i - 2])
+                project_unit(order[i])
+            if i >= 1:
+                finish_unit(order[i - 1])

@@ -25,20 +25,25 @@ NB = 2
 TAPS = 2 * NB + 1
 LN_EPS = 1e-5
 
-V_SETS = 5
+V_SETS = 4
 V_TOKENS = V_SETS * P
 PE_TILES = 12
 PE_STEP = 120
 PE_FIRST = TOKENS - PE_TILES * PE_STEP
+SHORT = PE_TILES
+SHORT_TOKENS = PE_FIRST - V_TOKENS
+WINDOWS = PE_TILES + 1
 BIAS_ROW = P - 1
 V_BUFS = 3
 Z_WIDTH = P + 2 * NB
-Z_ROW = (PE_TILES + 1) * Z_WIDTH
+Z_ROW = (WINDOWS + 1) * Z_WIDTH
 
 FLOPS = 2 * TOKENS * D * D
 
-GPSIMD_SETS = (0, 1, 2, 3, 4)
-GPSIMD_TILES = (0, 2, 4, 6, 8)
+G_PERIOD = 2
+G_TAKES = 1
+G_LAST = 14
+ORDER = "s0 s1 s2 s-2 s-1 w12 w0 w1 w2 s3 w3 w4 w5 s4 w6 w7 w8 s5 w9 w10 w11"
 
 
 def tile_crosssliceattention_pb_kernel(tc, x, Wv_words, Wv_scales, bv, attn_band, gamma, beta, out):
@@ -71,13 +76,17 @@ def tile_crosssliceattention_pb_kernel(tc, x, Wv_words, Wv_scales, bv, attn_band
         nc.vector.memset(w_scales[:].rearrange("p g n -> p (g n)").bitcast(I32), 0)
         band_w_bf = keep.tile([P, PE_TILES, TAPS], BF16, name="band_w_bf")
         nc.vector.memset(band_w_bf[:], 0.0)
-        z_rows = keep.tile([P, PE_TILES + 1, Z_WIDTH], F32, name="z_rows")
+        band_s_bf = keep.tile([P, TAPS], BF16, name="band_s_bf")
+        nc.vector.memset(band_s_bf[:], 0.0)
+        z_rows = keep.tile([P, WINDOWS + 1, Z_WIDTH], F32, name="z_rows")
         nc.vector.memset(z_rows[:], 0.0)
 
         x_set = {}
         for r in range(-NB, V_SETS + NB):
             x_set[r] = keep.tile([P, D], BF16, name="x_set%d" % (r + NB))
-        x_win = [keep.tile([P, D], BF16, name="x_win%d" % t) for t in range(PE_TILES)]
+        x_win = [keep.tile([P, D], BF16, name="x_win%d" % t) for t in range(WINDOWS)]
+        mix_T = keep.tile([P, F_BLOCKS, P], F32, name="mix_T")
+        nc.gpsimd.memset(mix_T[:], 0.0)
         for r in range(-NB, 0):
             nc.gpsimd.memset(x_set[r][0:1, :], 0.0)
         nc.gpsimd.memset(x_win[PE_TILES - 1][:], 0.0)
@@ -93,8 +102,11 @@ def tile_crosssliceattention_pb_kernel(tc, x, Wv_words, Wv_scales, bv, attn_band
                 src = x_rows[V_SETS : V_TOKENS + V_SETS].rearrange("(p r) d -> p r d", r=V_SETS)[:, r - V_SETS, :]
                 nc.sync.dma_start(out=x_set[r][:], in_=src)
 
+        def first_row(t):
+            return V_TOKENS if t == SHORT else PE_FIRST - NB + PE_STEP * t
+
         def load_window(t):
-            first = PE_FIRST - NB + PE_STEP * t
+            first = first_row(t)
             rows = min(P, TOKENS - first)
             whole = rows - rows % 16
             nc.sync.dma_start(out=x_win[t][0:whole, :], in_=x_rows[first : first + whole, :])
@@ -104,9 +116,19 @@ def tile_crosssliceattention_pb_kernel(tc, x, Wv_words, Wv_scales, bv, attn_band
         band_v_bf = keep.tile([P, V_SETS, TAPS], BF16, name="band_v_bf")
         nc.sync.dma_start(out=band_v_bf[:], in_=band_rows[0:V_TOKENS].rearrange("(p r) j -> p r j", r=V_SETS))
         nc.sync.dma_start(
-            out=band_w_bf[NB : NB + PE_STEP, :, :], in_=band_rows[PE_FIRST:TOKENS].rearrange("(t m) j -> m t j", m=PE_STEP)
+            out=band_w_bf[NB : NB + PE_STEP, :, :],
+            in_=band_rows[PE_FIRST:TOKENS].rearrange("(t m) j -> m t j", m=PE_STEP),
         )
-        load_set(0)
+        nc.sync.dma_start(out=band_s_bf[0:SHORT_TOKENS, :], in_=band_rows[V_TOKENS:PE_FIRST, :])
+        order = [("set" if word[0] == "s" else "win", int(word[1:])) for word in ORDER.split()]
+
+        def load_unit(unit):
+            if unit[0] == "set":
+                load_set(unit[1])
+            else:
+                load_window(unit[1])
+
+        load_unit(order[0])
         for quad in range(4):
             nc.sync.dma_start(
                 out=w_scales[32 * quad : 32 * quad + 4, :, :].bitcast(I32),
@@ -118,31 +140,30 @@ def tile_crosssliceattention_pb_kernel(tc, x, Wv_words, Wv_scales, bv, attn_band
         nc.sync.dma_start(out=bias_bf[:], in_=bv.partition_broadcast(P))
 
         nc.vector.tensor_copy(out=z_rows[:, 0:PE_TILES, 0:TAPS], in_=band_w_bf[:])
-        a_sum_w = keep.tile([P, PE_TILES], F32, name="a_sum_w")
-        nc.vector.tensor_reduce(out=a_sum_w[:], in_=z_rows[:, 0:PE_TILES, 0:TAPS], axis=AXIS.X, op=ALU.add)
-        nc.sync.dma_start(
+        nc.vector.tensor_copy(out=z_rows[:, SHORT, 0:TAPS], in_=band_s_bf[:])
+        a_sum_w = keep.tile([P, WINDOWS], F32, name="a_sum_w")
+        nc.vector.tensor_reduce(out=a_sum_w[:], in_=z_rows[:, 0:WINDOWS, 0:TAPS], axis=AXIS.X, op=ALU.add)
+        nc.gpsimd.dma_start(
             out=out_flat[scratch_base : scratch_base + P * Z_ROW].rearrange("(m w) -> m w", w=Z_ROW),
             in_=z_rows[:].rearrange("m t c -> m (t c)"),
         )
-        for r in (1, 2, -2, -1):
-            load_set(r)
-        a_tok = keep.tile([P, PE_TILES, P], F32, name="a_tok")
+        for unit in order[1:5]:
+            load_unit(unit)
+        a_tok = keep.tile([P, WINDOWS, P], F32, name="a_tok")
         skewed = out_flat[scratch_base + NB : scratch_base + NB + P * (Z_ROW - 1)].rearrange("(m w) -> m w", w=Z_ROW - 1)
-        nc.sync.dma_start(
-            out=a_tok[:], in_=skewed[:, 0 : PE_TILES * Z_WIDTH].rearrange("m (t c) -> m t c", c=Z_WIDTH)[:, :, 0:P]
+        nc.gpsimd.dma_start(
+            out=a_tok[:], in_=skewed[:, 0 : WINDOWS * Z_WIDTH].rearrange("m (t c) -> m t c", c=Z_WIDTH)[:, :, 0:P]
         )
         nc.sync.dma_start(out=gb_rows[0:F_BLOCKS, :], in_=gamma.rearrange("(b f) -> b f", f=P))
         nc.sync.dma_start(out=gb_rows[F_BLOCKS : 2 * F_BLOCKS, :], in_=beta.rearrange("(b f) -> b f", f=P))
-        for r in (3, 4, 5, 6):
-            load_set(r)
-        load_window(0)
-        load_window(1)
+        for unit in order[5:9]:
+            load_unit(unit)
         gamma_bf = keep.tile([P, D], BF16, name="gamma_bf")
         nc.sync.dma_start(out=gamma_bf[:], in_=gamma.partition_broadcast(P))
         beta_bf = keep.tile([P, D], BF16, name="beta_bf")
         nc.sync.dma_start(out=beta_bf[:], in_=beta.partition_broadcast(P))
-        for t in range(2, PE_TILES):
-            load_window(t)
+        for unit in order[9:]:
+            load_unit(unit)
 
         band_v = keep.tile([P, V_SETS, TAPS], F32, name="band_v")
         nc.vector.tensor_copy(out=band_v[:], in_=band_v_bf[:])
@@ -154,10 +175,11 @@ def tile_crosssliceattention_pb_kernel(tc, x, Wv_words, Wv_scales, bv, attn_band
             nc.gpsimd.tensor_copy(out=v_sb[i][96:P, :], in_=bias_bf[96:P, :])
 
         acc = [keep.tile([P, D], F32, name="acc%d" % d) for d in range(V_SETS)]
-        o_win = [keep.tile([P, D], F32, name="o_win%d" % t) for t in range(PE_TILES)]
+        o_win = [keep.tile([P, D], F32, name="o_win%d" % t) for t in range(WINDOWS)]
         sums_v = [keep.tile([P, HALVES], F32, name="sums_v%d" % d) for d in range(V_SETS)]
-        sums_w = [keep.tile([P, HALVES], F32, name="sums_w%d" % t) for t in range(PE_TILES)]
-        a_T = keep.tile([P, PE_TILES, P], F32, name="a_T")
+        sums_w = [keep.tile([P, HALVES], F32, name="sums_w%d" % t) for t in range(WINDOWS)]
+        a_T = keep.tile([P, WINDOWS, P], F32, name="a_T")
+        v_sb_of = {}
         taps_added = [[0] * V_SETS for h in range(HALVES)]
         spread = []
         grouped_of = {}
@@ -178,11 +200,12 @@ def tile_crosssliceattention_pb_kernel(tc, x, Wv_words, Wv_scales, bv, attn_band
             nc.vector.tensor_copy(out=gb_col[:], in_=gb_ps[:, 0 : 2 * F_BLOCKS])
 
         def transpose_bands(psum_xt):
-            for q in range(PE_TILES // 4):
+            for q in range(0, WINDOWS, 4):
+                n = min(4, WINDOWS - q)
                 at_ps = psum_xt.tile([P, 4, P], F32, name="at_ps", tag="xt")
-                for i in range(4):
-                    nc.tensor.transpose(at_ps[:, i, :], a_tok[:, 4 * q + i, :], ident[:])
-                nc.scalar.copy(out=a_T[:, 4 * q : 4 * q + 4, :], in_=at_ps[:])
+                for i in range(n):
+                    nc.tensor.transpose(at_ps[:, i, :], a_tok[:, q + i, :], ident[:])
+                nc.scalar.copy(out=a_T[:, q : q + n, :], in_=at_ps[:, 0:n, :])
 
         def x_of(unit):
             return x_set[unit[1]] if unit[0] == "set" else x_win[unit[1]]
@@ -213,6 +236,8 @@ def tile_crosssliceattention_pb_kernel(tc, x, Wv_words, Wv_scales, bv, attn_band
             x_codes, x_scales = quantised_of[unit]
             pool = psum_vv if unit[0] == "set" else psum_vw
             banks = []
+            if unit[0] == "win":
+                v_sb_of[unit[1]] = v_sb[len(v_sb_of) % V_BUFS]
             for h in range(HALVES):
                 v_ps = pool.tile([P, BANK], F32, name="v_ps")
                 for g in range(K_GROUPS):
@@ -227,7 +252,7 @@ def tile_crosssliceattention_pb_kernel(tc, x, Wv_words, Wv_scales, bv, attn_band
                     )
                 banks.append(v_ps)
                 if unit[0] == "win":
-                    nc.scalar.copy(out=v_sb[unit[1] % V_BUFS][0:BIAS_ROW, BANK * h : BANK * (h + 1)], in_=v_ps[0:BIAS_ROW, :])
+                    nc.scalar.copy(out=v_sb_of[unit[1]][0:BIAS_ROW, BANK * h : BANK * (h + 1)], in_=v_ps[0:BIAS_ROW, :])
             v_of[unit] = banks
 
         def add_taps(r):
@@ -246,11 +271,32 @@ def tile_crosssliceattention_pb_kernel(tc, x, Wv_words, Wv_scales, bv, attn_band
                     )
                     taps_added[h][d] += 1
 
+        def mix_short_window():
+            per_bank = F_BLOCKS // HALVES
+            for h in range(HALVES):
+                mix_T_ps = psum_mix.tile([P, per_bank, SHORT_TOKENS], F32, name="mix_T_ps", tag="mix_ps")
+                for q in range(per_bank):
+                    b = per_bank * h + q
+                    nc.tensor.matmul(
+                        out=mix_T_ps[:, q, :],
+                        lhsT=v_sb_of[SHORT][:, P * b : P * (b + 1)],
+                        rhs=a_T[:, SHORT, 0:SHORT_TOKENS],
+                        start=True,
+                        stop=True,
+                    )
+                nc.scalar.copy(out=mix_T[:, per_bank * h : per_bank * (h + 1), 0:SHORT_TOKENS], in_=mix_T_ps[:])
+
         def mix_window(t):
+            if t == SHORT:
+                mix_short_window()
             for h in range(HALVES):
                 cols = slice(BANK * h, BANK * (h + 1))
                 mix_ps = psum_mix.tile([P, BANK], F32, name="mix_ps")
-                nc.tensor.matmul(out=mix_ps[:], lhsT=a_T[:, t, :], rhs=v_sb[t % V_BUFS][:, cols], start=True, stop=True)
+                if t == SHORT:
+                    for q in range(BANK // P):
+                        nc.tensor.transpose(mix_ps[:, P * q : P * (q + 1)], mix_T[:, (BANK // P) * h + q, :], ident[:])
+                else:
+                    nc.tensor.matmul(out=mix_ps[:], lhsT=a_T[:, t, :], rhs=v_sb_of[t][:, cols], start=True, stop=True)
                 nc.vector.scalar_tensor_tensor(
                     out=o_win[t][:, cols],
                     in0=mix_ps[:],
@@ -281,31 +327,32 @@ def tile_crosssliceattention_pb_kernel(tc, x, Wv_words, Wv_scales, bv, attn_band
                 nc.vector.scalar_tensor_tensor(out=o[:], in0=o[:], scalar=neg_mean[:], in1=gamma_ps[:], op0=ALU.add, op1=ALU.mult)
                 nc.vector.scalar_tensor_tensor(out=o[:], in0=o[:], scalar=rstd[:], in1=beta_ps[:], op0=ALU.mult, op1=ALU.add)
 
+        finished = []
+
+        def to_gpsimd():
+            n = len(finished)
+            finished.append(n)
+            return n % G_PERIOD < G_TAKES and n < G_LAST
+
         def finish_unit(unit):
             if unit[0] == "set":
                 add_taps(unit[1])
                 for d in range(V_SETS):
                     if taps_added[HALVES - 1][d] == TAPS:
                         taps_added[HALVES - 1][d] += 1
-                        normalise(acc[d], sums_v[d], d in GPSIMD_SETS)
+                        normalise(acc[d], sums_v[d], to_gpsimd())
                         nc.sync.dma_start(
                             out=out_rows[0:V_TOKENS].rearrange("(p r) d -> p r d", r=V_SETS)[:, d, :], in_=acc[d][:]
                         )
             else:
                 t = unit[1]
                 mix_window(t)
-                normalise(o_win[t], sums_w[t], t in GPSIMD_TILES)
-                first = max(PE_FIRST + PE_STEP * t, V_TOKENS)
-                last = PE_FIRST + PE_STEP * (t + 1)
-                row = first - (PE_FIRST - NB + PE_STEP * t)
-                nc.sync.dma_start(out=out_rows[first:last, :], in_=o_win[t][row : row + last - first, :])
+                normalise(o_win[t], sums_w[t], to_gpsimd())
+                row = 0 if t == SHORT else NB
+                rows = SHORT_TOKENS if t == SHORT else PE_STEP
+                first = first_row(t) + row
+                nc.sync.dma_start(out=out_rows[first : first + rows, :], in_=o_win[t][row : row + rows, :])
 
-        order = [("set", r) for r in (0, 1, 2, -2, -1)]
-        later_sets = [3, 4, 5, 6]
-        for t in range(PE_TILES):
-            order.append(("win", t))
-            if t % 2 == 1 and later_sets:
-                order.append(("set", later_sets.pop(0)))
 
         groups = [order[0:1]] + [order[i : i + 2] for i in range(1, len(order), 2)]
         start_sums()

@@ -82,25 +82,15 @@ def tile_crosssliceattention_pb_kernel(tc, x, Wv_words, Wv_scales, bv, attn_band
         nc.vector.memset(z_rows[:], 0.0)
 
         x_set = {}
-        for r in range(-NB, V_SETS + NB):
-            x_set[r] = keep.tile([P, D], BF16, name="x_set%d" % (r + NB))
+        for r in range(V_SETS):
+            x_set[r] = keep.tile([P, D], BF16, name="x_set%d" % r)
         x_win = [keep.tile([P, D], BF16, name="x_win%d" % t) for t in range(WINDOWS)]
         mix_T = keep.tile([P, F_BLOCKS, P], F32, name="mix_T")
         nc.gpsimd.memset(mix_T[:], 0.0)
-        for r in range(-NB, 0):
-            nc.gpsimd.memset(x_set[r][0:1, :], 0.0)
         nc.gpsimd.memset(x_win[PE_TILES - 1][:], 0.0)
 
         def load_set(r):
-            if r < 0:
-                src = x_rows[0 : V_TOKENS - V_SETS].rearrange("(p r) d -> p r d", r=V_SETS)[:, r + V_SETS, :]
-                nc.sync.dma_start(out=x_set[r][1:113, :], in_=src[0:112, :])
-                nc.sync.dma_start(out=x_set[r][113:P, :], in_=src[112 : P - 1, :])
-            elif r < V_SETS:
-                nc.sync.dma_start(out=x_set[r][:], in_=x_rows[0:V_TOKENS].rearrange("(p r) d -> p r d", r=V_SETS)[:, r, :])
-            else:
-                src = x_rows[V_SETS : V_TOKENS + V_SETS].rearrange("(p r) d -> p r d", r=V_SETS)[:, r - V_SETS, :]
-                nc.sync.dma_start(out=x_set[r][:], in_=src)
+            nc.sync.dma_start(out=x_set[r][:], in_=x_rows[0:V_TOKENS].rearrange("(p r) d -> p r d", r=V_SETS)[:, r, :])
 
         def first_row(t):
             return V_TOKENS if t == SHORT else PE_FIRST - NB + PE_STEP * t
@@ -121,6 +111,7 @@ def tile_crosssliceattention_pb_kernel(tc, x, Wv_words, Wv_scales, bv, attn_band
         )
         nc.sync.dma_start(out=band_s_bf[0:SHORT_TOKENS, :], in_=band_rows[V_TOKENS:PE_FIRST, :])
         order = [("set" if word[0] == "s" else "win", int(word[1:])) for word in ORDER.split()]
+        made = [("set", r) for r in range(V_SETS)] + [unit for unit in order if unit[0] == "win"]
 
         def load_unit(unit):
             if unit[0] == "set":
@@ -128,7 +119,7 @@ def tile_crosssliceattention_pb_kernel(tc, x, Wv_words, Wv_scales, bv, attn_band
             else:
                 load_window(unit[1])
 
-        load_unit(order[0])
+        load_unit(made[0])
         for quad in range(4):
             nc.sync.dma_start(
                 out=w_scales[32 * quad : 32 * quad + 4, :, :].bitcast(I32),
@@ -147,7 +138,7 @@ def tile_crosssliceattention_pb_kernel(tc, x, Wv_words, Wv_scales, bv, attn_band
             out=out_flat[scratch_base : scratch_base + P * Z_ROW].rearrange("(m w) -> m w", w=Z_ROW),
             in_=z_rows[:].rearrange("m t c -> m (t c)"),
         )
-        for unit in order[1:5]:
+        for unit in made[1:5]:
             load_unit(unit)
         a_tok = keep.tile([P, WINDOWS, P], F32, name="a_tok")
         skewed = out_flat[scratch_base + NB : scratch_base + NB + P * (Z_ROW - 1)].rearrange("(m w) -> m w", w=Z_ROW - 1)
@@ -156,13 +147,13 @@ def tile_crosssliceattention_pb_kernel(tc, x, Wv_words, Wv_scales, bv, attn_band
         )
         nc.sync.dma_start(out=gb_rows[0:F_BLOCKS, :], in_=gamma.rearrange("(b f) -> b f", f=P))
         nc.sync.dma_start(out=gb_rows[F_BLOCKS : 2 * F_BLOCKS, :], in_=beta.rearrange("(b f) -> b f", f=P))
-        for unit in order[5:9]:
+        for unit in made[5:9]:
             load_unit(unit)
         gamma_bf = keep.tile([P, D], BF16, name="gamma_bf")
         nc.sync.dma_start(out=gamma_bf[:], in_=gamma.partition_broadcast(P))
         beta_bf = keep.tile([P, D], BF16, name="beta_bf")
         nc.sync.dma_start(out=beta_bf[:], in_=beta.partition_broadcast(P))
-        for unit in order[9:]:
+        for unit in made[9:]:
             load_unit(unit)
 
         band_v = keep.tile([P, V_SETS, TAPS], F32, name="band_v")
@@ -221,9 +212,33 @@ def tile_crosssliceattention_pb_kernel(tc, x, Wv_words, Wv_scales, bv, attn_band
                 nc.scalar.copy(out=grouped[:, i].bitcast(F32), in_=xt[:].rearrange("q g u t -> q g t u"))
             grouped_of[n] = grouped
 
+        moved_codes = keep.tile([P, 2 * NB, K_GROUPS, P], U32, name="moved_codes", align_bytes=64)
+        moved_scales = keep.tile([P, 2 * NB, K_GROUPS, P], U8, name="moved_scales", align_bytes=64)
+        nc.vector.memset(moved_codes[:, 0:NB, :, 0:1].bitcast(I32), 0)
+        nc.vector.memset(moved_codes[:, NB : 2 * NB, :, P - 1 : P].bitcast(I32), 0)
+        nc.vector.memset(moved_scales[:].rearrange("q i g t -> q (i g t)").bitcast(I32), 0)
+
+        def move_codes(r):
+            x_codes, x_scales = quantised_of[("set", r)]
+            if r >= V_SETS - NB:
+                i, to, start = r - (V_SETS - NB), r - V_SETS, (1, 0)
+            else:
+                i, to, start = NB + r, r + V_SETS, (0, 1)
+            if r >= NB and r < V_SETS - NB:
+                return
+            nc.gpsimd.tensor_copy(
+                out=moved_codes[:, i, :, start[0] : start[0] + P - 1], in_=x_codes[:, :, start[1] : start[1] + P - 1]
+            )
+            nc.gpsimd.tensor_copy(
+                out=moved_scales[:, i, :, start[0] : start[0] + P - 1], in_=x_scales[:, :, start[1] : start[1] + P - 1]
+            )
+            quantised_of[("set", to)] = (moved_codes[:, i], moved_scales[:, i])
+
         def quantise_units(n, units):
             x_codes = keep.tile([P, len(units), K_GROUPS, P], U32, name="x_codes%d" % n, align_bytes=64)
             x_scales = keep.tile([P, len(units), K_GROUPS, P], U8, name="x_scales%d" % n, align_bytes=64)
+            if units[0][0] == "set" or units[-1][0] == "set":
+                nc.vector.memset(x_scales[:].rearrange("q i g t -> q (i g t)").bitcast(I32), 0)
             nc.vector.quantize_mx(
                 out=x_codes[:].rearrange("q i g t -> q (i g t)").bitcast(FP8X4),
                 scales=x_scales[:].rearrange("q i g t -> q (i g t)"),
@@ -231,6 +246,8 @@ def tile_crosssliceattention_pb_kernel(tc, x, Wv_words, Wv_scales, bv, attn_band
             )
             for i, unit in enumerate(units):
                 quantised_of[unit] = (x_codes[:, i], x_scales[:, i])
+                if unit[0] == "set":
+                    move_codes(unit[1])
 
         def project_unit(unit):
             x_codes, x_scales = quantised_of[unit]
@@ -354,7 +371,7 @@ def tile_crosssliceattention_pb_kernel(tc, x, Wv_words, Wv_scales, bv, attn_band
                 nc.sync.dma_start(out=out_rows[first : first + rows, :], in_=o_win[t][row : row + rows, :])
 
 
-        groups = [order[0:1]] + [order[i : i + 2] for i in range(1, len(order), 2)]
+        groups = [made[0:1]] + [made[i : i + 2] for i in range(1, len(made), 2)]
         start_sums()
         with tc.psum_pool(name="psum_xt", bufs=2) as psum_xt:
             for n in range(len(groups) + 1):

@@ -43,6 +43,7 @@ FLOPS = 2 * TOKENS * D * D
 G_PERIOD = 2
 G_TAKES = 1
 G_LAST = 14
+MOVE_AHEAD = 2
 ORDER = "s0 s1 s2 s-2 s-1 w12 w0 w1 w2 s3 w3 w4 w5 s4 w6 w7 w8 s5 w9 w10 w11"
 
 
@@ -86,8 +87,8 @@ def tile_crosssliceattention_pb_kernel(tc, x, Wv_words, Wv_scales, bv, attn_band
             x_set[r] = keep.tile([P, D], BF16, name="x_set%d" % r)
         x_win = [keep.tile([P, D], BF16, name="x_win%d" % t) for t in range(WINDOWS)]
         mix_T = keep.tile([P, F_BLOCKS, P], F32, name="mix_T")
-        nc.gpsimd.memset(mix_T[:], 0.0)
-        nc.gpsimd.memset(x_win[PE_TILES - 1][:], 0.0)
+        nc.vector.memset(mix_T[:, :, SHORT_TOKENS:P], 0.0)
+        nc.vector.memset(x_win[PE_TILES - 1][96:P, :], 0.0)
 
         def load_set(r):
             nc.sync.dma_start(out=x_set[r][:], in_=x_rows[0:V_TOKENS].rearrange("(p r) d -> p r d", r=V_SETS)[:, r, :])
@@ -163,7 +164,7 @@ def tile_crosssliceattention_pb_kernel(tc, x, Wv_words, Wv_scales, bv, attn_band
         nc.vector.tensor_copy(out=a_tok[:, :, BIAS_ROW : BIAS_ROW + 1], in_=a_sum_w[:].unsqueeze(2))
         v_sb = [keep.tile([P, D], F32, name="v_sb%d" % i) for i in range(V_BUFS)]
         for i in range(V_BUFS):
-            nc.gpsimd.tensor_copy(out=v_sb[i][96:P, :], in_=bias_bf[96:P, :])
+            nc.scalar.copy(out=v_sb[i][96:P, :], in_=bias_bf[96:P, :])
 
         acc = [keep.tile([P, D], F32, name="acc%d" % d) for d in range(V_SETS)]
         o_win = [keep.tile([P, D], F32, name="o_win%d" % t) for t in range(WINDOWS)]
@@ -218,14 +219,12 @@ def tile_crosssliceattention_pb_kernel(tc, x, Wv_words, Wv_scales, bv, attn_band
         nc.vector.memset(moved_codes[:, NB : 2 * NB, :, P - 1 : P].bitcast(I32), 0)
         nc.vector.memset(moved_scales[:].rearrange("q i g t -> q (i g t)").bitcast(I32), 0)
 
-        def move_codes(r):
-            x_codes, x_scales = quantised_of[("set", r)]
-            if r >= V_SETS - NB:
-                i, to, start = r - (V_SETS - NB), r - V_SETS, (1, 0)
+        def move_codes(to):
+            if to < 0:
+                r, i, start = to + V_SETS, to + NB, (1, 0)
             else:
-                i, to, start = NB + r, r + V_SETS, (0, 1)
-            if r >= NB and r < V_SETS - NB:
-                return
+                r, i, start = to - V_SETS, to - V_SETS + NB, (0, 1)
+            x_codes, x_scales = quantised_of[("set", r)]
             nc.gpsimd.tensor_copy(
                 out=moved_codes[:, i, :, start[0] : start[0] + P - 1], in_=x_codes[:, :, start[1] : start[1] + P - 1]
             )
@@ -246,8 +245,6 @@ def tile_crosssliceattention_pb_kernel(tc, x, Wv_words, Wv_scales, bv, attn_band
             )
             for i, unit in enumerate(units):
                 quantised_of[unit] = (x_codes[:, i], x_scales[:, i])
-                if unit[0] == "set":
-                    move_codes(unit[1])
 
         def project_unit(unit):
             x_codes, x_scales = quantised_of[unit]
@@ -391,8 +388,11 @@ def tile_crosssliceattention_pb_kernel(tc, x, Wv_words, Wv_scales, bv, attn_band
                 beta_ps[:, P * b : P * (b + 1)], gb_col[:, F_BLOCKS + b : F_BLOCKS + b + 1].to_broadcast([P, P]), ident_bf[:]
             )
         spread.extend([gamma_ps, beta_ps])
-        for i in range(len(order) + 1):
-            if i < len(order):
+        for i in range(-MOVE_AHEAD, len(order) + 1):
+            ahead = order[i + MOVE_AHEAD] if i + MOVE_AHEAD < len(order) else made[0]
+            if ahead not in made:
+                move_codes(ahead[1])
+            if 0 <= i < len(order):
                 project_unit(order[i])
             if i >= 1:
                 finish_unit(order[i - 1])

@@ -87,8 +87,8 @@ def tile_crosssliceattention_pb_kernel(tc, x, Wv_words, Wv_scales, bv, attn_band
             x_set[r] = keep.tile([P, D], BF16, name="x_set%d" % r)
         x_win = [keep.tile([P, D], BF16, name="x_win%d" % t) for t in range(WINDOWS)]
         mix_T = keep.tile([P, F_BLOCKS, P], F32, name="mix_T")
-        nc.vector.memset(mix_T[:, :, SHORT_TOKENS:P], 0.0)
-        nc.vector.memset(x_win[PE_TILES - 1][96:P, :], 0.0)
+        nc.gpsimd.memset(mix_T[:, :, SHORT_TOKENS:P], 0.0)
+        nc.gpsimd.memset(x_win[PE_TILES - 1][96:P, :], 0.0)
 
         def load_set(r):
             nc.sync.dma_start(out=x_set[r][:], in_=x_rows[0:V_TOKENS].rearrange("(p r) d -> p r d", r=V_SETS)[:, r, :])
@@ -164,7 +164,7 @@ def tile_crosssliceattention_pb_kernel(tc, x, Wv_words, Wv_scales, bv, attn_band
         nc.vector.tensor_copy(out=a_tok[:, :, BIAS_ROW : BIAS_ROW + 1], in_=a_sum_w[:].unsqueeze(2))
         v_sb = [keep.tile([P, D], F32, name="v_sb%d" % i) for i in range(V_BUFS)]
         for i in range(V_BUFS):
-            nc.scalar.copy(out=v_sb[i][96:P, :], in_=bias_bf[96:P, :])
+            nc.gpsimd.tensor_scalar(out=v_sb[i][96:P, :], in0=bias_bf[96:P, :], scalar1=1.0, scalar2=0.0, op0=ALU.mult, op1=ALU.add)
 
         acc = [keep.tile([P, D], F32, name="acc%d" % d) for d in range(V_SETS)]
         o_win = [keep.tile([P, D], F32, name="o_win%d" % t) for t in range(WINDOWS)]

@@ -44,7 +44,7 @@ G_PERIOD = 2
 G_TAKES = 1
 G_LAST = 14
 MOVE_AHEAD = 2
-ORDER = "s0 s1 s2 s-2 s-1 w12 w0 w1 w2 s3 w3 w4 w5 s4 w6 w7 w8 s5 w9 w10 w11"
+ORDER = "s0 s1 s2 s3 w12 w0 w1 w2 s-2 s-1 w3 w4 w5 s4 w6 w7 w8 s5 w9 w10 w11"
 
 
 def tile_crosssliceattention_pb_kernel(tc, x, Wv_words, Wv_scales, bv, attn_band, gamma, beta, out):

@@ -321,7 +321,7 @@ def tile_crosssliceattention_pb_kernel(tc, x, Wv_words, Wv_scales, bv, attn_band
                     accum_out=sums_w[t][:, h : h + 1],
                 )
 
-        def normalise(o, row_sums, on_gpsimd):
+        def measure(o, row_sums, on_gpsimd):
             halves = stats.tile([P, HALVES], F32, name="halves")
             neg_mean = stats.tile([P, 1], F32, name="neg_mean")
             nc.scalar.activation(out=halves[:], in_=row_sums[:], func=ACT.Identity, scale=-1.0 / D, accum_out=neg_mean[:])
@@ -334,6 +334,10 @@ def tile_crosssliceattention_pb_kernel(tc, x, Wv_words, Wv_scales, bv, attn_band
                 shift = stats.tile([P, 1], F32, name="shift")
                 nc.scalar.activation(out=shift[:], in_=neg_mean[:], func=ACT.Copy, scale=rstd[:])
                 nc.scalar.activation(out=o[:], in_=o[:], func=ACT.Identity, bias=shift[:], scale=rstd[:])
+            return neg_mean, rstd
+
+        def scale_and_shift(o, neg_mean, rstd, on_gpsimd):
+            if on_gpsimd:
                 nc.gpsimd.tensor_tensor(out=o[:], in0=o[:], in1=gamma_bf[:], op=ALU.mult)
                 nc.gpsimd.tensor_tensor(out=o[:], in0=o[:], in1=beta_bf[:], op=ALU.add)
             else:
@@ -342,6 +346,14 @@ def tile_crosssliceattention_pb_kernel(tc, x, Wv_words, Wv_scales, bv, attn_band
                 nc.vector.scalar_tensor_tensor(out=o[:], in0=o[:], scalar=rstd[:], in1=beta_ps[:], op0=ALU.mult, op1=ALU.add)
 
         finished = []
+        measured = []
+
+        def store_measured(count):
+            for o, neg_mean, rstd, on_gpsimd, rows_out, rows_in in measured[0:count]:
+                scale_and_shift(o, neg_mean, rstd, on_gpsimd)
+                nc.sync.dma_start(out=rows_out, in_=rows_in)
+            for n in range(count):
+                measured.remove(measured[0])
 
         def to_gpsimd():
             n = len(finished)
@@ -354,21 +366,24 @@ def tile_crosssliceattention_pb_kernel(tc, x, Wv_words, Wv_scales, bv, attn_band
                 for d in range(V_SETS):
                     if taps_added[HALVES - 1][d] == TAPS:
                         taps_added[HALVES - 1][d] += 1
-                        normalise(acc[d], sums_v[d], to_gpsimd())
-                        nc.sync.dma_start(
-                            out=out_rows[0:V_TOKENS].rearrange("(p r) d -> p r d", r=V_SETS)[:, d, :], in_=acc[d][:]
-                        )
+                        on_gpsimd = to_gpsimd()
+                        neg_mean, rstd = measure(acc[d], sums_v[d], on_gpsimd)
+                        rows_out = out_rows[0:V_TOKENS].rearrange("(p r) d -> p r d", r=V_SETS)[:, d, :]
+                        measured.append((acc[d], neg_mean, rstd, on_gpsimd, rows_out, acc[d][:]))
             else:
                 t = unit[1]
                 mix_window(t)
-                normalise(o_win[t], sums_w[t], to_gpsimd())
+                on_gpsimd = to_gpsimd()
+                neg_mean, rstd = measure(o_win[t], sums_w[t], on_gpsimd)
                 row = 0 if t == SHORT else NB
                 rows = SHORT_TOKENS if t == SHORT else PE_STEP
                 first = first_row(t) + row
-                nc.sync.dma_start(out=out_rows[first : first + rows, :], in_=o_win[t][row : row + rows, :])
+                measured.append(
+                    (o_win[t], neg_mean, rstd, on_gpsimd, out_rows[first : first + rows, :], o_win[t][row : row + rows, :])
+                )
 
 
-        groups = [made[0:1]] + [made[i : i + 2] for i in range(1, len(made), 2)]
+        groups = [made[0:1]] + [made[i : i + 4] for i in range(1, len(made), 4)]
         start_sums()
         with tc.psum_pool(name="psum_xt", bufs=2) as psum_xt:
             for n in range(len(groups) + 1):
@@ -376,7 +391,7 @@ def tile_crosssliceattention_pb_kernel(tc, x, Wv_words, Wv_scales, bv, attn_band
                     transpose_units(psum_xt, n, groups[n])
                 if n >= 1:
                     quantise_units(n - 1, groups[n - 1])
-                if n == 3:
+                if n == 2:
                     transpose_bands(psum_xt)
                     transpose_gain_and_shift(psum_xt)
         psum_gb = ctx.enter_context(tc.psum_pool(name="psum_gb", bufs=1))
@@ -395,4 +410,7 @@ def tile_crosssliceattention_pb_kernel(tc, x, Wv_words, Wv_scales, bv, attn_band
             if 0 <= i < len(order):
                 project_unit(order[i])
             if i >= 1:
+                earlier = len(measured)
                 finish_unit(order[i - 1])
+                store_measured(earlier)
+        store_measured(len(measured))

@@ -34,17 +34,31 @@ SHORT = PE_TILES
 SHORT_TOKENS = PE_FIRST - V_TOKENS
 WINDOWS = PE_TILES + 1
 BIAS_ROW = P - 1
-V_BUFS = 3
+V_BUFS = 4
 Z_WIDTH = P + 2 * NB
 Z_ROW = (WINDOWS + 1) * Z_WIDTH
 
 FLOPS = 2 * TOKENS * D * D
 
-G_PERIOD = 2
-G_TAKES = 1
-G_LAST = 14
-MOVE_AHEAD = 2
-ORDER = "s0 s1 s2 s3 w12 w0 w1 w2 s-2 s-1 w3 w4 w5 s4 w6 w7 w8 s5 w9 w10 w11"
+MOVE_AHEAD = 3
+ORDER = "s0 s1 w0 s2 w1 s3 w2 w3 s-2 w4 s-1 w5 w6 s4 w7 w8 s5 w9 w10 w12 w11"
+QUANTISE_TOGETHER = (1, 2, 2, 4, 4, 4)
+G_LAST = 15
+BANDS_AT = 3
+LEAD = 8
+QLAG = 1
+BLAG = 2
+ALAG = 3
+SLAG = 2
+TICK = "N P B Q H M S A T"
+G_PER = 2
+G_TAKE = 1
+XT_BUFS = 2
+START = 5
+GBASE = False
+OWN = ()
+G_FIRST = 0
+V_BANKS = 2
 
 
 def tile_crosssliceattention_pb_kernel(tc, x, Wv_words, Wv_scales, bv, attn_band, gamma, beta, out):
@@ -59,7 +73,7 @@ def tile_crosssliceattention_pb_kernel(tc, x, Wv_words, Wv_scales, bv, attn_band
         keep = ctx.enter_context(tc.tile_pool(name="keep", bufs=1))
         stage = ctx.enter_context(tc.tile_pool(name="stage", bufs=3))
         stats = ctx.enter_context(tc.tile_pool(name="stats", bufs=4))
-        psum_vv = ctx.enter_context(tc.psum_pool(name="psum_vv", bufs=2))
+        psum_vv = ctx.enter_context(tc.psum_pool(name="psum_vv", bufs=V_BANKS))
         psum_vw = ctx.enter_context(tc.psum_pool(name="psum_vw", bufs=2))
         psum_mix = ctx.enter_context(tc.psum_pool(name="psum_mix", bufs=2))
 
@@ -104,15 +118,8 @@ def tile_crosssliceattention_pb_kernel(tc, x, Wv_words, Wv_scales, bv, attn_band
             if whole < rows:
                 nc.sync.dma_start(out=x_win[t][whole:rows, :], in_=x_rows[first + whole : first + rows, :])
 
-        band_v_bf = keep.tile([P, V_SETS, TAPS], BF16, name="band_v_bf")
-        nc.sync.dma_start(out=band_v_bf[:], in_=band_rows[0:V_TOKENS].rearrange("(p r) j -> p r j", r=V_SETS))
-        nc.sync.dma_start(
-            out=band_w_bf[NB : NB + PE_STEP, :, :],
-            in_=band_rows[PE_FIRST:TOKENS].rearrange("(t m) j -> m t j", m=PE_STEP),
-        )
-        nc.sync.dma_start(out=band_s_bf[0:SHORT_TOKENS, :], in_=band_rows[V_TOKENS:PE_FIRST, :])
         order = [("set" if word[0] == "s" else "win", int(word[1:])) for word in ORDER.split()]
-        made = [("set", r) for r in range(V_SETS)] + [unit for unit in order if unit[0] == "win"]
+        made = [unit for unit in order if unit[0] == "win" or 0 <= unit[1] < V_SETS]
 
         def load_unit(unit):
             if unit[0] == "set":
@@ -121,6 +128,11 @@ def tile_crosssliceattention_pb_kernel(tc, x, Wv_words, Wv_scales, bv, attn_band
                 load_window(unit[1])
 
         load_unit(made[0])
+        nc.sync.dma_start(
+            out=band_w_bf[NB : NB + PE_STEP, :, :],
+            in_=band_rows[PE_FIRST:TOKENS].rearrange("(t m) j -> m t j", m=PE_STEP),
+        )
+        nc.sync.dma_start(out=band_s_bf[0:SHORT_TOKENS, :], in_=band_rows[V_TOKENS:PE_FIRST, :])
         for quad in range(4):
             nc.sync.dma_start(
                 out=w_scales[32 * quad : 32 * quad + 4, :, :].bitcast(I32),
@@ -128,8 +140,12 @@ def tile_crosssliceattention_pb_kernel(tc, x, Wv_words, Wv_scales, bv, attn_band
             )
         w_words = keep.tile([P, K_GROUPS, 2 * D], U8, name="w_words", align_bytes=64)
         nc.sync.dma_start(out=w_words[:].bitcast(I32), in_=Wv_words.rearrange("g p n -> p g n").bitcast(I32))
+        band_v_bf = keep.tile([P, V_SETS, TAPS], BF16, name="band_v_bf")
+        nc.sync.dma_start(out=band_v_bf[:], in_=band_rows[0:V_TOKENS].rearrange("(p r) j -> p r j", r=V_SETS))
         bias_bf = keep.tile([P, D], BF16, name="bias_bf")
         nc.sync.dma_start(out=bias_bf[:], in_=bv.partition_broadcast(P))
+        for unit in made[1:3]:
+            load_unit(unit)
 
         nc.vector.tensor_copy(out=z_rows[:, 0:PE_TILES, 0:TAPS], in_=band_w_bf[:])
         nc.vector.tensor_copy(out=z_rows[:, SHORT, 0:TAPS], in_=band_s_bf[:])
@@ -139,17 +155,15 @@ def tile_crosssliceattention_pb_kernel(tc, x, Wv_words, Wv_scales, bv, attn_band
             out=out_flat[scratch_base : scratch_base + P * Z_ROW].rearrange("(m w) -> m w", w=Z_ROW),
             in_=z_rows[:].rearrange("m t c -> m (t c)"),
         )
-        for unit in made[1:5]:
-            load_unit(unit)
         a_tok = keep.tile([P, WINDOWS, P], F32, name="a_tok")
         skewed = out_flat[scratch_base + NB : scratch_base + NB + P * (Z_ROW - 1)].rearrange("(m w) -> m w", w=Z_ROW - 1)
         nc.gpsimd.dma_start(
             out=a_tok[:], in_=skewed[:, 0 : WINDOWS * Z_WIDTH].rearrange("m (t c) -> m t c", c=Z_WIDTH)[:, :, 0:P]
         )
+        for unit in made[3:9]:
+            load_unit(unit)
         nc.sync.dma_start(out=gb_rows[0:F_BLOCKS, :], in_=gamma.rearrange("(b f) -> b f", f=P))
         nc.sync.dma_start(out=gb_rows[F_BLOCKS : 2 * F_BLOCKS, :], in_=beta.rearrange("(b f) -> b f", f=P))
-        for unit in made[5:9]:
-            load_unit(unit)
         gamma_bf = keep.tile([P, D], BF16, name="gamma_bf")
         nc.sync.dma_start(out=gamma_bf[:], in_=gamma.partition_broadcast(P))
         beta_bf = keep.tile([P, D], BF16, name="beta_bf")
@@ -161,7 +175,6 @@ def tile_crosssliceattention_pb_kernel(tc, x, Wv_words, Wv_scales, bv, attn_band
         nc.vector.tensor_copy(out=band_v[:], in_=band_v_bf[:])
         a_sum_v = keep.tile([P, V_SETS], F32, name="a_sum_v")
         nc.vector.tensor_reduce(out=a_sum_v[:], in_=band_v[:], axis=AXIS.X, op=ALU.add)
-        nc.vector.tensor_copy(out=a_tok[:, :, BIAS_ROW : BIAS_ROW + 1], in_=a_sum_w[:].unsqueeze(2))
         v_sb = [keep.tile([P, D], F32, name="v_sb%d" % i) for i in range(V_BUFS)]
         for i in range(V_BUFS):
             nc.gpsimd.tensor_scalar(out=v_sb[i][96:P, :], in0=bias_bf[96:P, :], scalar1=1.0, scalar2=0.0, op0=ALU.mult, op1=ALU.add)
@@ -178,8 +191,12 @@ def tile_crosssliceattention_pb_kernel(tc, x, Wv_words, Wv_scales, bv, attn_band
         quantised_of = {}
         v_of = {}
 
-        def start_sums():
-            for d in range(V_SETS):
+        def start_sums(sets):
+            for d in sets:
+                if GBASE:
+                    nc.gpsimd.tensor_scalar(out=acc[d][:], in0=bias_bf[:], scalar1=a_sum_v[:, d : d + 1], scalar2=0.0, op0=ALU.mult, op1=ALU.add)
+                    nc.gpsimd.tensor_tensor(out=acc[d][:], in0=acc[d][:], in1=x_set[d][:], op=ALU.add)
+                    continue
                 nc.vector.scalar_tensor_tensor(
                     out=acc[d][:], in0=bias_bf[:], scalar=a_sum_v[:, d : d + 1], in1=x_set[d][:], op0=ALU.mult, op1=ALU.add
                 )
@@ -192,6 +209,7 @@ def tile_crosssliceattention_pb_kernel(tc, x, Wv_words, Wv_scales, bv, attn_band
             nc.vector.tensor_copy(out=gb_col[:], in_=gb_ps[:, 0 : 2 * F_BLOCKS])
 
         def transpose_bands(psum_xt):
+            nc.vector.tensor_copy(out=a_tok[:, :, BIAS_ROW : BIAS_ROW + 1], in_=a_sum_w[:].unsqueeze(2))
             for q in range(0, WINDOWS, 4):
                 n = min(4, WINDOWS - q)
                 at_ps = psum_xt.tile([P, 4, P], F32, name="at_ps", tag="xt")
@@ -274,6 +292,12 @@ def tile_crosssliceattention_pb_kernel(tc, x, Wv_words, Wv_scales, bv, attn_band
                 cols = slice(BANK * h, BANK * (h + 1))
                 for d in range(max(r - NB, 0), min(r + NB, V_SETS - 1) + 1):
                     j = r - d + NB
+                    if (d, j) in OWN:
+                        part = stage.tile([P, BANK], F32, name="part")
+                        nc.scalar.activation(out=part[:], in_=v_of[("set", r)][h][:], func=ACT.Copy, scale=band_v[:, d, j : j + 1])
+                        nc.gpsimd.tensor_tensor(out=acc[d][:, cols], in0=acc[d][:, cols], in1=part[:], op=ALU.add)
+                        taps_added[h][d] += 1
+                        continue
                     nc.vector.scalar_tensor_tensor(
                         out=acc[d][:, cols],
                         in0=v_of[("set", r)][h][:],
@@ -300,6 +324,8 @@ def tile_crosssliceattention_pb_kernel(tc, x, Wv_words, Wv_scales, bv, attn_band
                     )
                 nc.scalar.copy(out=mix_T[:, per_bank * h : per_bank * (h + 1), 0:SHORT_TOKENS], in_=mix_T_ps[:])
 
+        mix_of = {}
+
         def mix_window(t):
             if t == SHORT:
                 mix_short_window()
@@ -311,9 +337,14 @@ def tile_crosssliceattention_pb_kernel(tc, x, Wv_words, Wv_scales, bv, attn_band
                         nc.tensor.transpose(mix_ps[:, P * q : P * (q + 1)], mix_T[:, (BANK // P) * h + q, :], ident[:])
                 else:
                     nc.tensor.matmul(out=mix_ps[:], lhsT=a_T[:, t, :], rhs=v_sb_of[t][:, cols], start=True, stop=True)
+                mix_of[(t, h)] = mix_ps
+
+        def add_x(t):
+            for h in range(HALVES):
+                cols = slice(BANK * h, BANK * (h + 1))
                 nc.vector.scalar_tensor_tensor(
                     out=o_win[t][:, cols],
-                    in0=mix_ps[:],
+                    in0=mix_of[(t, h)][:],
                     scalar=1.0,
                     in1=x_win[t][:, cols],
                     op0=ALU.mult,
@@ -321,79 +352,143 @@ def tile_crosssliceattention_pb_kernel(tc, x, Wv_words, Wv_scales, bv, attn_band
                     accum_out=sums_w[t][:, h : h + 1],
                 )
 
-        def measure(o, row_sums, on_gpsimd):
+        def measure(o, row_sums):
             halves = stats.tile([P, HALVES], F32, name="halves")
             neg_mean = stats.tile([P, 1], F32, name="neg_mean")
             nc.scalar.activation(out=halves[:], in_=row_sums[:], func=ACT.Identity, scale=-1.0 / D, accum_out=neg_mean[:])
             squares = stage.tile([P, D], BF16, name="squares")
             sum_sq = stats.tile([P, 1], F32, name="sum_sq")
             nc.scalar.activation(out=squares[:], in_=o[:], func=ACT.Square, bias=neg_mean[:], scale=1.0, accum_out=sum_sq[:])
+            return neg_mean, sum_sq
+
+        def normalise(o, neg_mean, sum_sq, on_gpsimd):
             rstd = stats.tile([P, 1], F32, name="rstd")
             nc.scalar.activation(out=rstd[:], in_=sum_sq[:], func=ACT.Abs_reciprocal_sqrt, bias=eps_col[:], scale=1.0 / D)
             if on_gpsimd:
                 shift = stats.tile([P, 1], F32, name="shift")
                 nc.scalar.activation(out=shift[:], in_=neg_mean[:], func=ACT.Copy, scale=rstd[:])
                 nc.scalar.activation(out=o[:], in_=o[:], func=ACT.Identity, bias=shift[:], scale=rstd[:])
-            return neg_mean, rstd
-
-        def scale_and_shift(o, neg_mean, rstd, on_gpsimd):
-            if on_gpsimd:
                 nc.gpsimd.tensor_tensor(out=o[:], in0=o[:], in1=gamma_bf[:], op=ALU.mult)
                 nc.gpsimd.tensor_tensor(out=o[:], in0=o[:], in1=beta_bf[:], op=ALU.add)
-            else:
-                gamma_ps, beta_ps = spread
-                nc.vector.scalar_tensor_tensor(out=o[:], in0=o[:], scalar=neg_mean[:], in1=gamma_ps[:], op0=ALU.add, op1=ALU.mult)
-                nc.vector.scalar_tensor_tensor(out=o[:], in0=o[:], scalar=rstd[:], in1=beta_ps[:], op0=ALU.mult, op1=ALU.add)
+            return rstd
 
         finished = []
         measured = []
-
-        def store_measured(count):
-            for o, neg_mean, rstd, on_gpsimd, rows_out, rows_in in measured[0:count]:
-                scale_and_shift(o, neg_mean, rstd, on_gpsimd)
-                nc.sync.dma_start(out=rows_out, in_=rows_in)
-            for n in range(count):
-                measured.remove(measured[0])
+        scaled = []
+        count = []
 
         def to_gpsimd():
-            n = len(finished)
-            finished.append(n)
-            return n % G_PERIOD < G_TAKES and n < G_LAST
+            n = len(count)
+            count.append(n)
+            return not spread or ((n < G_FIRST or n % G_PER < G_TAKE) and n < G_LAST)
 
-        def finish_unit(unit):
+        def sum_unit(unit):
             if unit[0] == "set":
                 add_taps(unit[1])
                 for d in range(V_SETS):
                     if taps_added[HALVES - 1][d] == TAPS:
                         taps_added[HALVES - 1][d] += 1
-                        on_gpsimd = to_gpsimd()
-                        neg_mean, rstd = measure(acc[d], sums_v[d], on_gpsimd)
                         rows_out = out_rows[0:V_TOKENS].rearrange("(p r) d -> p r d", r=V_SETS)[:, d, :]
-                        measured.append((acc[d], neg_mean, rstd, on_gpsimd, rows_out, acc[d][:]))
+                        finished.append((acc[d], sums_v[d], rows_out, acc[d][:]))
             else:
                 t = unit[1]
-                mix_window(t)
-                on_gpsimd = to_gpsimd()
-                neg_mean, rstd = measure(o_win[t], sums_w[t], on_gpsimd)
+                add_x(t)
                 row = 0 if t == SHORT else NB
                 rows = SHORT_TOKENS if t == SHORT else PE_STEP
                 first = first_row(t) + row
-                measured.append(
-                    (o_win[t], neg_mean, rstd, on_gpsimd, out_rows[first : first + rows, :], o_win[t][row : row + rows, :])
-                )
+                finished.append((o_win[t], sums_w[t], out_rows[first : first + rows, :], o_win[t][row : row + rows, :]))
 
+        def shift_scaled():
+            while scaled:
+                o, rstd, rows_out, rows_in = scaled[0]
+                scaled.remove(scaled[0])
+                gamma_ps, beta_ps = spread
+                nc.vector.scalar_tensor_tensor(out=o[:], in0=o[:], scalar=rstd[:], in1=beta_ps[:], op0=ALU.mult, op1=ALU.add)
+                nc.sync.dma_start(out=rows_out, in_=rows_in)
 
-        groups = [made[0:1]] + [made[i : i + 4] for i in range(1, len(made), 4)]
-        start_sums()
-        with tc.psum_pool(name="psum_xt", bufs=2) as psum_xt:
-            for n in range(len(groups) + 1):
-                if n < len(groups):
-                    transpose_units(psum_xt, n, groups[n])
-                if n >= 1:
-                    quantise_units(n - 1, groups[n - 1])
-                if n == 2:
-                    transpose_bands(psum_xt)
-                    transpose_gain_and_shift(psum_xt)
+        def measure_finished_one():
+            if finished:
+                o, row_sums, rows_out, rows_in = finished[0]
+                finished.remove(finished[0])
+                neg_mean, sum_sq = measure(o, row_sums)
+                measured.append((o, neg_mean, sum_sq, rows_out, rows_in))
+
+        def scale_measured():
+            while measured:
+                o, neg_mean, sum_sq, rows_out, rows_in = measured[0]
+                measured.remove(measured[0])
+                on_gpsimd = to_gpsimd()
+                rstd = normalise(o, neg_mean, sum_sq, on_gpsimd)
+                if on_gpsimd:
+                    nc.sync.dma_start(out=rows_out, in_=rows_in)
+                else:
+                    gamma_ps, beta_ps = spread
+                    nc.vector.scalar_tensor_tensor(
+                        out=o[:], in0=o[:], scalar=neg_mean[:], in1=gamma_ps[:], op0=ALU.add, op1=ALU.mult
+                    )
+                    scaled.append((o, rstd, rows_out, rows_in))
+
+        steps = []
+
+        def at(k):
+            return order[k] if 0 <= k < len(order) else ("none", 0)
+
+        def step():
+            i = len(steps) - START
+            steps.append(i)
+            waiting = len(finished)
+            for stage in TICK.split():
+                if stage == "T":
+                    while len(turned) < len(groups) and (not turned or sum(len(groups[n]) for n in turned) < made_before(i + LEAD)):
+                        n = len(turned)
+                        turned.append(n)
+                        turned_at.append(i)
+                        transpose_units(psum_xt, n, groups[n])
+                    if i >= BANDS_AT and not banded:
+                        banded.append(1)
+                        transpose_bands(psum_xt)
+                        transpose_gain_and_shift(psum_xt)
+                if stage == "Q":
+                    while len(quantised) < len(turned) and turned_at[len(quantised)] <= i - QLAG:
+                        n = len(quantised)
+                        quantised.append(n)
+                        quantise_units(n, groups[n])
+                        start_sums([unit[1] for unit in groups[n] if unit[0] == "set"])
+                if stage == "P":
+                    for ahead in order[max(i, 0) : max(i, 0) + MOVE_AHEAD + 1]:
+                        if ahead not in made and ahead not in quantised_of:
+                            move_codes(ahead[1])
+                    if at(i)[0] != "none":
+                        project_unit(at(i))
+                if stage == "B" and at(i - BLAG)[0] == "win":
+                    mix_window(at(i - BLAG)[1])
+                if stage == "A" and at(i - ALAG)[0] == "win":
+                    sum_unit(at(i - ALAG))
+                if stage == "S" and at(i - SLAG)[0] == "set":
+                    sum_unit(at(i - SLAG))
+                if stage == "M":
+                    for tile in range(waiting):
+                        measure_finished_one()
+                if stage == "N":
+                    scale_measured()
+                if stage == "H":
+                    shift_scaled()
+
+        def made_before(k):
+            return len([unit for unit in order[0 : max(k, 0) + 1] if unit in made])
+
+        groups = []
+        for n in QUANTISE_TOGETHER:
+            done = sum(len(group) for group in groups)
+            groups.append(made[done : done + n])
+        turned = []
+        turned_at = []
+        quantised = []
+        banded = []
+        with tc.psum_pool(name="psum_xt", bufs=XT_BUFS) as psum_xt:
+            while len(quantised) < len(groups) or not banded:
+                step()
+        assert banded
         psum_gb = ctx.enter_context(tc.psum_pool(name="psum_gb", bufs=1))
         gamma_ps = psum_gb.tile([P, D], BF16, name="gamma_ps")
         beta_ps = psum_gb.tile([P, D], BF16, name="beta_ps")
@@ -403,14 +498,5 @@ def tile_crosssliceattention_pb_kernel(tc, x, Wv_words, Wv_scales, bv, attn_band
                 beta_ps[:, P * b : P * (b + 1)], gb_col[:, F_BLOCKS + b : F_BLOCKS + b + 1].to_broadcast([P, P]), ident_bf[:]
             )
         spread.extend([gamma_ps, beta_ps])
-        for i in range(-MOVE_AHEAD, len(order) + 1):
-            ahead = order[i + MOVE_AHEAD] if i + MOVE_AHEAD < len(order) else made[0]
-            if ahead not in made:
-                move_codes(ahead[1])
-            if 0 <= i < len(order):
-                project_unit(order[i])
-            if i >= 1:
-                earlier = len(measured)
-                finish_unit(order[i - 1])
-                store_measured(earlier)
-        store_measured(len(measured))
+        while steps[-1] < len(order) + ALAG or finished or measured or scaled:
+            step()

@@ -55,6 +55,8 @@ G_PER = 2
 G_TAKE = 1
 XT_BUFS = 2
 START = 5
+LOADS_1 = 6
+LOADS_2 = 9
 GBASE = False
 OWN = ()
 G_FIRST = 0
@@ -81,12 +83,6 @@ def tile_crosssliceattention_pb_kernel(tc, x, Wv_words, Wv_scales, bv, attn_band
         masks.make_identity(nc, ident[:])
         ident_bf = keep.tile([P, P], BF16, name="ident_bf")
         masks.make_identity(nc, ident_bf[:])
-        gb_rows = keep.tile([P, P], BF16, name="gb_rows")
-        nc.vector.memset(gb_rows[:], 0.0)
-        eps_col = keep.tile([P, 1], F32, name="eps_col")
-        nc.vector.memset(eps_col[:], LN_EPS)
-        warm = keep.tile([P, 1], F32, name="warm")
-        nc.scalar.activation(out=warm[:], in_=eps_col[:], func=ACT.Abs_reciprocal_sqrt)
         w_scales = keep.tile([P, K_GROUPS, D], U8, name="w_scales", align_bytes=64)
         nc.vector.memset(w_scales[:].rearrange("p g n -> p (g n)").bitcast(I32), 0)
         band_w_bf = keep.tile([P, PE_TILES, TAPS], BF16, name="band_w_bf")
@@ -95,6 +91,12 @@ def tile_crosssliceattention_pb_kernel(tc, x, Wv_words, Wv_scales, bv, attn_band
         nc.vector.memset(band_s_bf[:], 0.0)
         z_rows = keep.tile([P, WINDOWS + 1, Z_WIDTH], F32, name="z_rows")
         nc.vector.memset(z_rows[:], 0.0)
+        eps_col = keep.tile([P, 1], F32, name="eps_col")
+        nc.vector.memset(eps_col[:], LN_EPS)
+        warm = keep.tile([P, 1], F32, name="warm")
+        nc.scalar.activation(out=warm[:], in_=eps_col[:], func=ACT.Abs_reciprocal_sqrt)
+        gb_rows = keep.tile([P, P], BF16, name="gb_rows")
+        nc.vector.memset(gb_rows[:], 0.0)
 
         x_set = {}
         for r in range(V_SETS):
@@ -128,39 +130,43 @@ def tile_crosssliceattention_pb_kernel(tc, x, Wv_words, Wv_scales, bv, attn_band
                 load_window(unit[1])
 
         load_unit(made[0])
-        nc.sync.dma_start(
-            out=band_w_bf[NB : NB + PE_STEP, :, :],
-            in_=band_rows[PE_FIRST:TOKENS].rearrange("(t m) j -> m t j", m=PE_STEP),
-        )
-        nc.sync.dma_start(out=band_s_bf[0:SHORT_TOKENS, :], in_=band_rows[V_TOKENS:PE_FIRST, :])
+        w_words = keep.tile([P, K_GROUPS, 2 * D], U8, name="w_words", align_bytes=64)
+        nc.sync.dma_start(out=w_words[:].bitcast(I32), in_=Wv_words.rearrange("g p n -> p g n").bitcast(I32))
         for quad in range(4):
             nc.sync.dma_start(
                 out=w_scales[32 * quad : 32 * quad + 4, :, :].bitcast(I32),
                 in_=Wv_scales[:, 4 * quad : 4 * quad + 4, :].rearrange("g r n -> r g n").bitcast(I32),
             )
-        w_words = keep.tile([P, K_GROUPS, 2 * D], U8, name="w_words", align_bytes=64)
-        nc.sync.dma_start(out=w_words[:].bitcast(I32), in_=Wv_words.rearrange("g p n -> p g n").bitcast(I32))
+        for unit in made[1:3]:
+            load_unit(unit)
+        nc.sync.dma_start(
+            out=band_w_bf[NB : NB + PE_STEP, :, :],
+            in_=band_rows[PE_FIRST:TOKENS].rearrange("(t m) j -> m t j", m=PE_STEP),
+        )
+        nc.sync.dma_start(out=band_s_bf[0:SHORT_TOKENS, :], in_=band_rows[V_TOKENS:PE_FIRST, :])
         band_v_bf = keep.tile([P, V_SETS, TAPS], BF16, name="band_v_bf")
         nc.sync.dma_start(out=band_v_bf[:], in_=band_rows[0:V_TOKENS].rearrange("(p r) j -> p r j", r=V_SETS))
         bias_bf = keep.tile([P, D], BF16, name="bias_bf")
         nc.sync.dma_start(out=bias_bf[:], in_=bv.partition_broadcast(P))
-        for unit in made[1:3]:
+        for unit in made[3:LOADS_1]:
             load_unit(unit)
 
         nc.vector.tensor_copy(out=z_rows[:, 0:PE_TILES, 0:TAPS], in_=band_w_bf[:])
         nc.vector.tensor_copy(out=z_rows[:, SHORT, 0:TAPS], in_=band_s_bf[:])
-        a_sum_w = keep.tile([P, WINDOWS], F32, name="a_sum_w")
-        nc.vector.tensor_reduce(out=a_sum_w[:], in_=z_rows[:, 0:WINDOWS, 0:TAPS], axis=AXIS.X, op=ALU.add)
-        nc.gpsimd.dma_start(
+        nc.sync.dma_start(
             out=out_flat[scratch_base : scratch_base + P * Z_ROW].rearrange("(m w) -> m w", w=Z_ROW),
             in_=z_rows[:].rearrange("m t c -> m (t c)"),
         )
         a_tok = keep.tile([P, WINDOWS, P], F32, name="a_tok")
         skewed = out_flat[scratch_base + NB : scratch_base + NB + P * (Z_ROW - 1)].rearrange("(m w) -> m w", w=Z_ROW - 1)
-        nc.gpsimd.dma_start(
+        for unit in made[LOADS_1:LOADS_2]:
+            load_unit(unit)
+        nc.sync.dma_start(
             out=a_tok[:], in_=skewed[:, 0 : WINDOWS * Z_WIDTH].rearrange("m (t c) -> m t c", c=Z_WIDTH)[:, :, 0:P]
         )
-        for unit in made[3:9]:
+        a_sum_w = keep.tile([P, WINDOWS], F32, name="a_sum_w")
+        nc.vector.tensor_reduce(out=a_sum_w[:], in_=z_rows[:, 0:WINDOWS, 0:TAPS], axis=AXIS.X, op=ALU.add)
+        for unit in made[LOADS_2:12]:
             load_unit(unit)
         nc.sync.dma_start(out=gb_rows[0:F_BLOCKS, :], in_=gamma.rearrange("(b f) -> b f", f=P))
         nc.sync.dma_start(out=gb_rows[F_BLOCKS : 2 * F_BLOCKS, :], in_=beta.rearrange("(b f) -> b f", f=P))
@@ -168,7 +174,7 @@ def tile_crosssliceattention_pb_kernel(tc, x, Wv_words, Wv_scales, bv, attn_band
         nc.sync.dma_start(out=gamma_bf[:], in_=gamma.partition_broadcast(P))
         beta_bf = keep.tile([P, D], BF16, name="beta_bf")
         nc.sync.dma_start(out=beta_bf[:], in_=beta.partition_broadcast(P))
-        for unit in made[9:]:
+        for unit in made[12:]:
             load_unit(unit)
 
         band_v = keep.tile([P, V_SETS, TAPS], F32, name="band_v")

from contextlib import ExitStack

import concourse.masks as masks
import concourse.mybir as mybir

F32 = mybir.dt.float32
BF16 = mybir.dt.bfloat16
U8 = mybir.dt.uint8
U32 = mybir.dt.uint32
I32 = mybir.dt.int32
FP8X4 = mybir.dt.float8_e4m3fn_x4
FP4X4 = mybir.dt.float4_e2m1fn_x4
ACT = mybir.ActivationFunctionType
ALU = mybir.AluOpType
AXIS = mybir.AxisListType

P = 128
D = 1024
TOKENS = 4 * 512
K_GROUPS = D // 512
BANK = 512
HALVES = D // BANK
F_BLOCKS = D // P
NB = 2
TAPS = 2 * NB + 1
LN_EPS = 1e-5

V_SETS = 4
V_TOKENS = V_SETS * P
PE_TILES = 12
PE_STEP = 120
PE_FIRST = TOKENS - PE_TILES * PE_STEP
SHORT = PE_TILES
SHORT_TOKENS = PE_FIRST - V_TOKENS
WINDOWS = PE_TILES + 1
BIAS_ROW = P - 1
V_BUFS = 4
Z_WIDTH = P + 2 * NB
Z_ROW = (WINDOWS + 1) * Z_WIDTH

FLOPS = 2 * TOKENS * D * D

MOVE_AHEAD = 3
ORDER = "s0 s1 w0 s2 w1 s3 w2 w3 s-2 w4 s-1 w5 w6 s4 w7 w8 s5 w9 w10 w12 w11"
QUANTISE_TOGETHER = (1, 2, 2, 4, 4, 4)
G_LAST = 15
BANDS_AT = 3
LEAD = 8
QLAG = 1
BLAG = 2
ALAG = 3
SLAG = 2
TICK = "N P B Q H M S A T"
G_PER = 2
G_TAKE = 1
XT_BUFS = 2
START = 5
LOADS_1 = 6
LOADS_2 = 9
GBASE = False
OWN = ()
G_FIRST = 0
V_BANKS = 2


def tile_crosssliceattention_pb_kernel(tc, x, Wv_words, Wv_scales, bv, attn_band, gamma, beta, out):
    nc = tc.nc
    x_rows = x.flatten_outer_dims()
    out_rows = out.flatten_outer_dims()
    band_rows = attn_band.flatten_outer_dims()
    out_flat = out_rows.rearrange("s d -> (s d)")
    scratch_base = (TOKENS - (P * Z_ROW + D - 1) // D) * D

    with ExitStack() as ctx:
        keep = ctx.enter_context(tc.tile_pool(name="keep", bufs=1))
        stage = ctx.enter_context(tc.tile_pool(name="stage", bufs=3))
        stats = ctx.enter_context(tc.tile_pool(name="stats", bufs=4))
        psum_vv = ctx.enter_context(tc.psum_pool(name="psum_vv", bufs=V_BANKS))
        psum_vw = ctx.enter_context(tc.psum_pool(name="psum_vw", bufs=2))
        psum_mix = ctx.enter_context(tc.psum_pool(name="psum_mix", bufs=2))

        ident = keep.tile([P, P], F32, name="ident")
        masks.make_identity(nc, ident[:])
        ident_bf = keep.tile([P, P], BF16, name="ident_bf")
        masks.make_identity(nc, ident_bf[:])
        w_scales = keep.tile([P, K_GROUPS, D], U8, name="w_scales", align_bytes=64)
        nc.vector.memset(w_scales[:].rearrange("p g n -> p (g n)").bitcast(I32), 0)
        band_w_bf = keep.tile([P, PE_TILES, TAPS], BF16, name="band_w_bf")
        nc.vector.memset(band_w_bf[:], 0.0)
        band_s_bf = keep.tile([P, TAPS], BF16, name="band_s_bf")
        nc.vector.memset(band_s_bf[:], 0.0)
        z_rows = keep.tile([P, WINDOWS + 1, Z_WIDTH], F32, name="z_rows")
        nc.vector.memset(z_rows[:], 0.0)
        eps_col = keep.tile([P, 1], F32, name="eps_col")
        nc.vector.memset(eps_col[:], LN_EPS)
        warm = keep.tile([P, 1], F32, name="warm")
        nc.scalar.activation(out=warm[:], in_=eps_col[:], func=ACT.Abs_reciprocal_sqrt)
        gb_rows = keep.tile([P, P], BF16, name="gb_rows")
        nc.vector.memset(gb_rows[:], 0.0)

        x_set = {}
        for r in range(V_SETS):
            x_set[r] = keep.tile([P, D], BF16, name="x_set%d" % r)
        x_win = [keep.tile([P, D], BF16, name="x_win%d" % t) for t in range(WINDOWS)]
        mix_T = keep.tile([P, F_BLOCKS, P], F32, name="mix_T")
        nc.gpsimd.memset(mix_T[:, :, SHORT_TOKENS:P], 0.0)
        nc.gpsimd.memset(x_win[PE_TILES - 1][96:P, :], 0.0)

        def load_set(r):
            nc.sync.dma_start(out=x_set[r][:], in_=x_rows[0:V_TOKENS].rearrange("(p r) d -> p r d", r=V_SETS)[:, r, :])

        def first_row(t):
            return V_TOKENS if t == SHORT else PE_FIRST - NB + PE_STEP * t

        def load_window(t):
            first = first_row(t)
            rows = min(P, TOKENS - first)
            whole = rows - rows % 16
            nc.sync.dma_start(out=x_win[t][0:whole, :], in_=x_rows[first : first + whole, :])
            if whole < rows:
                nc.sync.dma_start(out=x_win[t][whole:rows, :], in_=x_rows[first + whole : first + rows, :])

        order = [("set" if word[0] == "s" else "win", int(word[1:])) for word in ORDER.split()]
        made = [unit for unit in order if unit[0] == "win" or 0 <= unit[1] < V_SETS]

        def load_unit(unit):
            if unit[0] == "set":
                load_set(unit[1])
            else:
                load_window(unit[1])

        load_unit(made[0])
        w_words = keep.tile([P, K_GROUPS, 2 * D], U8, name="w_words", align_bytes=64)
        nc.sync.dma_start(out=w_words[:].bitcast(I32), in_=Wv_words.rearrange("g p n -> p g n").bitcast(I32))
        for quad in range(4):
            nc.sync.dma_start(
                out=w_scales[32 * quad : 32 * quad + 4, :, :].bitcast(I32),
                in_=Wv_scales[:, 4 * quad : 4 * quad + 4, :].rearrange("g r n -> r g n").bitcast(I32),
            )
        for unit in made[1:3]:
            load_unit(unit)
        nc.sync.dma_start(
            out=band_w_bf[NB : NB + PE_STEP, :, :],
            in_=band_rows[PE_FIRST:TOKENS].rearrange("(t m) j -> m t j", m=PE_STEP),
        )
        nc.sync.dma_start(out=band_s_bf[0:SHORT_TOKENS, :], in_=band_rows[V_TOKENS:PE_FIRST, :])
        band_v_bf = keep.tile([P, V_SETS, TAPS], BF16, name="band_v_bf")
        nc.sync.dma_start(out=band_v_bf[:], in_=band_rows[0:V_TOKENS].rearrange("(p r) j -> p r j", r=V_SETS))
        bias_bf = keep.tile([P, D], BF16, name="bias_bf")
        nc.sync.dma_start(out=bias_bf[:], in_=bv.partition_broadcast(P))
        for unit in made[3:LOADS_1]:
            load_unit(unit)

        nc.vector.tensor_copy(out=z_rows[:, 0:PE_TILES, 0:TAPS], in_=band_w_bf[:])
        nc.vector.tensor_copy(out=z_rows[:, SHORT, 0:TAPS], in_=band_s_bf[:])
        nc.sync.dma_start(
            out=out_flat[scratch_base : scratch_base + P * Z_ROW].rearrange("(m w) -> m w", w=Z_ROW),
            in_=z_rows[:].rearrange("m t c -> m (t c)"),
        )
        a_tok = keep.tile([P, WINDOWS, P], F32, name="a_tok")
        skewed = out_flat[scratch_base + NB : scratch_base + NB + P * (Z_ROW - 1)].rearrange("(m w) -> m w", w=Z_ROW - 1)
        for unit in made[LOADS_1:LOADS_2]:
            load_unit(unit)
        nc.sync.dma_start(
            out=a_tok[:], in_=skewed[:, 0 : WINDOWS * Z_WIDTH].rearrange("m (t c) -> m t c", c=Z_WIDTH)[:, :, 0:P]
        )
        a_sum_w = keep.tile([P, WINDOWS], F32, name="a_sum_w")
        nc.vector.tensor_reduce(out=a_sum_w[:], in_=z_rows[:, 0:WINDOWS, 0:TAPS], axis=AXIS.X, op=ALU.add)
        for unit in made[LOADS_2:12]:
            load_unit(unit)
        nc.sync.dma_start(out=gb_rows[0:F_BLOCKS, :], in_=gamma.rearrange("(b f) -> b f", f=P))
        nc.sync.dma_start(out=gb_rows[F_BLOCKS : 2 * F_BLOCKS, :], in_=beta.rearrange("(b f) -> b f", f=P))
        gamma_bf = keep.tile([P, D], BF16, name="gamma_bf")
        nc.sync.dma_start(out=gamma_bf[:], in_=gamma.partition_broadcast(P))
        beta_bf = keep.tile([P, D], BF16, name="beta_bf")
        nc.sync.dma_start(out=beta_bf[:], in_=beta.partition_broadcast(P))
        for unit in made[12:]:
            load_unit(unit)

        band_v = keep.tile([P, V_SETS, TAPS], F32, name="band_v")
        nc.vector.tensor_copy(out=band_v[:], in_=band_v_bf[:])
        a_sum_v = keep.tile([P, V_SETS], F32, name="a_sum_v")
        nc.vector.tensor_reduce(out=a_sum_v[:], in_=band_v[:], axis=AXIS.X, op=ALU.add)
        v_sb = [keep.tile([P, D], F32, name="v_sb%d" % i) for i in range(V_BUFS)]
        for i in range(V_BUFS):
            nc.gpsimd.tensor_scalar(out=v_sb[i][96:P, :], in0=bias_bf[96:P, :], scalar1=1.0, scalar2=0.0, op0=ALU.mult, op1=ALU.add)

        acc = [keep.tile([P, D], F32, name="acc%d" % d) for d in range(V_SETS)]
        o_win = [keep.tile([P, D], F32, name="o_win%d" % t) for t in range(WINDOWS)]
        sums_v = [keep.tile([P, HALVES], F32, name="sums_v%d" % d) for d in range(V_SETS)]
        sums_w = [keep.tile([P, HALVES], F32, name="sums_w%d" % t) for t in range(WINDOWS)]
        a_T = keep.tile([P, WINDOWS, P], F32, name="a_T")
        v_sb_of = {}
        taps_added = [[0] * V_SETS for h in range(HALVES)]
        spread = []
        grouped_of = {}
        quantised_of = {}
        v_of = {}

        def start_sums(sets):
            for d in sets:
                if GBASE:
                    nc.gpsimd.tensor_scalar(out=acc[d][:], in0=bias_bf[:], scalar1=a_sum_v[:, d : d + 1], scalar2=0.0, op0=ALU.mult, op1=ALU.add)
                    nc.gpsimd.tensor_tensor(out=acc[d][:], in0=acc[d][:], in1=x_set[d][:], op=ALU.add)
                    continue
                nc.vector.scalar_tensor_tensor(
                    out=acc[d][:], in0=bias_bf[:], scalar=a_sum_v[:, d : d + 1], in1=x_set[d][:], op0=ALU.mult, op1=ALU.add
                )

        gb_col = keep.tile([P, 2 * F_BLOCKS], BF16, name="gb_col")

        def transpose_gain_and_shift(psum_xt):
            gb_ps = psum_xt.tile([P, P], BF16, name="gb_ps", tag="xt")
            nc.tensor.transpose(gb_ps[:], gb_rows[:], ident_bf[:])
            nc.vector.tensor_copy(out=gb_col[:], in_=gb_ps[:, 0 : 2 * F_BLOCKS])

        def transpose_bands(psum_xt):
            nc.vector.tensor_copy(out=a_tok[:, :, BIAS_ROW : BIAS_ROW + 1], in_=a_sum_w[:].unsqueeze(2))
            for q in range(0, WINDOWS, 4):
                n = min(4, WINDOWS - q)
                at_ps = psum_xt.tile([P, 4, P], F32, name="at_ps", tag="xt")
                for i in range(n):
                    nc.tensor.transpose(at_ps[:, i, :], a_tok[:, q + i, :], ident[:])
                nc.scalar.copy(out=a_T[:, q : q + n, :], in_=at_ps[:, 0:n, :])

        def x_of(unit):
            return x_set[unit[1]] if unit[0] == "set" else x_win[unit[1]]

        def transpose_units(psum_xt, n, units):
            grouped = stage.tile([P, len(units), K_GROUPS, P, 4], BF16, name="grouped", align_bytes=64)
            for i, unit in enumerate(units):
                x_words = x_of(unit)[:].bitcast(F32)
                xt = psum_xt.tile([P, K_GROUPS, 2, P], F32, name="xt", tag="xt")
                for g in range(K_GROUPS):
                    for u in range(2):
                        nc.tensor.transpose(xt[:, g, u, :], x_words[:, 256 * g + u : 256 * (g + 1) : 2], ident[:])
                nc.scalar.copy(out=grouped[:, i].bitcast(F32), in_=xt[:].rearrange("q g u t -> q g t u"))
            grouped_of[n] = grouped

        moved_codes = keep.tile([P, 2 * NB, K_GROUPS, P], U32, name="moved_codes", align_bytes=64)
        moved_scales = keep.tile([P, 2 * NB, K_GROUPS, P], U8, name="moved_scales", align_bytes=64)
        nc.vector.memset(moved_codes[:, 0:NB, :, 0:1].bitcast(I32), 0)
        nc.vector.memset(moved_codes[:, NB : 2 * NB, :, P - 1 : P].bitcast(I32), 0)
        nc.vector.memset(moved_scales[:].rearrange("q i g t -> q (i g t)").bitcast(I32), 0)

        def move_codes(to):
            if to < 0:
                r, i, start = to + V_SETS, to + NB, (1, 0)
            else:
                r, i, start = to - V_SETS, to - V_SETS + NB, (0, 1)
            x_codes, x_scales = quantised_of[("set", r)]
            nc.gpsimd.tensor_copy(
                out=moved_codes[:, i, :, start[0] : start[0] + P - 1], in_=x_codes[:, :, start[1] : start[1] + P - 1]
            )
            nc.gpsimd.tensor_copy(
                out=moved_scales[:, i, :, start[0] : start[0] + P - 1], in_=x_scales[:, :, start[1] : start[1] + P - 1]
            )
            quantised_of[("set", to)] = (moved_codes[:, i], moved_scales[:, i])

        def quantise_units(n, units):
            x_codes = keep.tile([P, len(units), K_GROUPS, P], U32, name="x_codes%d" % n, align_bytes=64)
            x_scales = keep.tile([P, len(units), K_GROUPS, P], U8, name="x_scales%d" % n, align_bytes=64)
            if units[0][0] == "set" or units[-1][0] == "set":
                nc.vector.memset(x_scales[:].rearrange("q i g t -> q (i g t)").bitcast(I32), 0)
            nc.vector.quantize_mx(
                out=x_codes[:].rearrange("q i g t -> q (i g t)").bitcast(FP8X4),
                scales=x_scales[:].rearrange("q i g t -> q (i g t)"),
                in_=grouped_of[n][:].rearrange("q i g t j -> q (i g t j)"),
            )
            for i, unit in enumerate(units):
                quantised_of[unit] = (x_codes[:, i], x_scales[:, i])

        def project_unit(unit):
            x_codes, x_scales = quantised_of[unit]
            pool = psum_vv if unit[0] == "set" else psum_vw
            banks = []
            if unit[0] == "win":
                v_sb_of[unit[1]] = v_sb[len(v_sb_of) % V_BUFS]
            for h in range(HALVES):
                v_ps = pool.tile([P, BANK], F32, name="v_ps")
                for g in range(K_GROUPS):
                    nc.tensor.matmul_mx(
                        out=v_ps[:],
                        lhsT=x_codes[:, g, :].bitcast(FP8X4),
                        lhsT_scale=x_scales[:, g, :],
                        rhs=w_words[:, g, 2 * BANK * h : 2 * BANK * (h + 1)].bitcast(FP4X4),
                        rhs_scale=w_scales[:, g, BANK * h : BANK * (h + 1)],
                        start=(g == 0),
                        stop=(g == K_GROUPS - 1),
                    )
                banks.append(v_ps)
                if unit[0] == "win":
                    nc.scalar.copy(out=v_sb_of[unit[1]][0:BIAS_ROW, BANK * h : BANK * (h + 1)], in_=v_ps[0:BIAS_ROW, :])
            v_of[unit] = banks

        def add_taps(r):
            for h in range(HALVES):
                cols = slice(BANK * h, BANK * (h + 1))
                for d in range(max(r - NB, 0), min(r + NB, V_SETS - 1) + 1):
                    j = r - d + NB
                    if (d, j) in OWN:
                        part = stage.tile([P, BANK], F32, name="part")
                        nc.scalar.activation(out=part[:], in_=v_of[("set", r)][h][:], func=ACT.Copy, scale=band_v[:, d, j : j + 1])
                        nc.gpsimd.tensor_tensor(out=acc[d][:, cols], in0=acc[d][:, cols], in1=part[:], op=ALU.add)
                        taps_added[h][d] += 1
                        continue
                    nc.vector.scalar_tensor_tensor(
                        out=acc[d][:, cols],
                        in0=v_of[("set", r)][h][:],
                        scalar=band_v[:, d, j : j + 1],
                        in1=acc[d][:, cols],
                        op0=ALU.mult,
                        op1=ALU.add,
                        accum_out=sums_v[d][:, h : h + 1] if taps_added[h][d] == TAPS - 1 else None,
                    )
                    taps_added[h][d] += 1

        def mix_short_window():
            per_bank = F_BLOCKS // HALVES
            for h in range(HALVES):
                mix_T_ps = psum_mix.tile([P, per_bank, SHORT_TOKENS], F32, name="mix_T_ps", tag="mix_ps")
                for q in range(per_bank):
                    b = per_bank * h + q
                    nc.tensor.matmul(
                        out=mix_T_ps[:, q, :],
                        lhsT=v_sb_of[SHORT][:, P * b : P * (b + 1)],
                        rhs=a_T[:, SHORT, 0:SHORT_TOKENS],
                        start=True,
                        stop=True,
                    )
                nc.scalar.copy(out=mix_T[:, per_bank * h : per_bank * (h + 1), 0:SHORT_TOKENS], in_=mix_T_ps[:])

        mix_of = {}

        def mix_window(t):
            if t == SHORT:
                mix_short_window()
            for h in range(HALVES):
                cols = slice(BANK * h, BANK * (h + 1))
                mix_ps = psum_mix.tile([P, BANK], F32, name="mix_ps")
                if t == SHORT:
                    for q in range(BANK // P):
                        nc.tensor.transpose(mix_ps[:, P * q : P * (q + 1)], mix_T[:, (BANK // P) * h + q, :], ident[:])
                else:
                    nc.tensor.matmul(out=mix_ps[:], lhsT=a_T[:, t, :], rhs=v_sb_of[t][:, cols], start=True, stop=True)
                mix_of[(t, h)] = mix_ps

        def add_x(t):
            for h in range(HALVES):
                cols = slice(BANK * h, BANK * (h + 1))
                nc.vector.scalar_tensor_tensor(
                    out=o_win[t][:, cols],
                    in0=mix_of[(t, h)][:],
                    scalar=1.0,
                    in1=x_win[t][:, cols],
                    op0=ALU.mult,
                    op1=ALU.add,
                    accum_out=sums_w[t][:, h : h + 1],
                )

        def measure(o, row_sums):
            halves = stats.tile([P, HALVES], F32, name="halves")
            neg_mean = stats.tile([P, 1], F32, name="neg_mean")
            nc.scalar.activation(out=halves[:], in_=row_sums[:], func=ACT.Identity, scale=-1.0 / D, accum_out=neg_mean[:])
            squares = stage.tile([P, D], BF16, name="squares")
            sum_sq = stats.tile([P, 1], F32, name="sum_sq")
            nc.scalar.activation(out=squares[:], in_=o[:], func=ACT.Square, bias=neg_mean[:], scale=1.0, accum_out=sum_sq[:])
            return neg_mean, sum_sq

        def normalise(o, neg_mean, sum_sq, on_gpsimd):
            rstd = stats.tile([P, 1], F32, name="rstd")
            nc.scalar.activation(out=rstd[:], in_=sum_sq[:], func=ACT.Abs_reciprocal_sqrt, bias=eps_col[:], scale=1.0 / D)
            if on_gpsimd:
                shift = stats.tile([P, 1], F32, name="shift")
                nc.scalar.activation(out=shift[:], in_=neg_mean[:], func=ACT.Copy, scale=rstd[:])
                nc.scalar.activation(out=o[:], in_=o[:], func=ACT.Identity, bias=shift[:], scale=rstd[:])
                nc.gpsimd.tensor_tensor(out=o[:], in0=o[:], in1=gamma_bf[:], op=ALU.mult)
                nc.gpsimd.tensor_tensor(out=o[:], in0=o[:], in1=beta_bf[:], op=ALU.add)
            return rstd

        finished = []
        measured = []
        scaled = []
        count = []

        def to_gpsimd():
            n = len(count)
            count.append(n)
            return not spread or ((n < G_FIRST or n % G_PER < G_TAKE) and n < G_LAST)

        def sum_unit(unit):
            if unit[0] == "set":
                add_taps(unit[1])
                for d in range(V_SETS):
                    if taps_added[HALVES - 1][d] == TAPS:
                        taps_added[HALVES - 1][d] += 1
                        rows_out = out_rows[0:V_TOKENS].rearrange("(p r) d -> p r d", r=V_SETS)[:, d, :]
                        finished.append((acc[d], sums_v[d], rows_out, acc[d][:]))
            else:
                t = unit[1]
                add_x(t)
                row = 0 if t == SHORT else NB
                rows = SHORT_TOKENS if t == SHORT else PE_STEP
                first = first_row(t) + row
                finished.append((o_win[t], sums_w[t], out_rows[first : first + rows, :], o_win[t][row : row + rows, :]))

        def shift_scaled():
            while scaled:
                o, rstd, rows_out, rows_in = scaled[0]
                scaled.remove(scaled[0])
                gamma_ps, beta_ps = spread
                nc.vector.scalar_tensor_tensor(out=o[:], in0=o[:], scalar=rstd[:], in1=beta_ps[:], op0=ALU.mult, op1=ALU.add)
                nc.sync.dma_start(out=rows_out, in_=rows_in)

        def measure_finished_one():
            if finished:
                o, row_sums, rows_out, rows_in = finished[0]
                finished.remove(finished[0])
                neg_mean, sum_sq = measure(o, row_sums)
                measured.append((o, neg_mean, sum_sq, rows_out, rows_in))

        def scale_measured():
            while measured:
                o, neg_mean, sum_sq, rows_out, rows_in = measured[0]
                measured.remove(measured[0])
                on_gpsimd = to_gpsimd()
                rstd = normalise(o, neg_mean, sum_sq, on_gpsimd)
                if on_gpsimd:
                    nc.sync.dma_start(out=rows_out, in_=rows_in)
                else:
                    gamma_ps, beta_ps = spread
                    nc.vector.scalar_tensor_tensor(
                        out=o[:], in0=o[:], scalar=neg_mean[:], in1=gamma_ps[:], op0=ALU.add, op1=ALU.mult
                    )
                    scaled.append((o, rstd, rows_out, rows_in))

        steps = []

        def at(k):
            return order[k] if 0 <= k < len(order) else ("none", 0)

        def step():
            i = len(steps) - START
            steps.append(i)
            waiting = len(finished)
            for stage in TICK.split():
                if stage == "T":
                    while len(turned) < len(groups) and (not turned or sum(len(groups[n]) for n in turned) < made_before(i + LEAD)):
                        n = len(turned)
                        turned.append(n)
                        turned_at.append(i)
                        transpose_units(psum_xt, n, groups[n])
                    if i >= BANDS_AT and not banded:
                        banded.append(1)
                        transpose_bands(psum_xt)
                        transpose_gain_and_shift(psum_xt)
                if stage == "Q":
                    while len(quantised) < len(turned) and turned_at[len(quantised)] <= i - QLAG:
                        n = len(quantised)
                        quantised.append(n)
                        quantise_units(n, groups[n])
                        start_sums([unit[1] for unit in groups[n] if unit[0] == "set"])
                if stage == "P":
                    for ahead in order[max(i, 0) : max(i, 0) + MOVE_AHEAD + 1]:
                        if ahead not in made and ahead not in quantised_of:
                            move_codes(ahead[1])
                    if at(i)[0] != "none":
                        project_unit(at(i))
                if stage == "B" and at(i - BLAG)[0] == "win":
                    mix_window(at(i - BLAG)[1])
                if stage == "A" and at(i - ALAG)[0] == "win":
                    sum_unit(at(i - ALAG))
                if stage == "S" and at(i - SLAG)[0] == "set":
                    sum_unit(at(i - SLAG))
                if stage == "M":
                    for tile in range(waiting):
                        measure_finished_one()
                if stage == "N":
                    scale_measured()
                if stage == "H":
                    shift_scaled()

        def made_before(k):
            return len([unit for unit in order[0 : max(k, 0) + 1] if unit in made])

        groups = []
        for n in QUANTISE_TOGETHER:
            done = sum(len(group) for group in groups)
            groups.append(made[done : done + n])
        turned = []
        turned_at = []
        quantised = []
        banded = []
        with tc.psum_pool(name="psum_xt", bufs=XT_BUFS) as psum_xt:
            while len(quantised) < len(groups) or not banded:
                step()
        assert banded
        psum_gb = ctx.enter_context(tc.psum_pool(name="psum_gb", bufs=1))
        gamma_ps = psum_gb.tile([P, D], BF16, name="gamma_ps")
        beta_ps = psum_gb.tile([P, D], BF16, name="beta_ps")
        for b in range(F_BLOCKS):
            nc.tensor.transpose(gamma_ps[:, P * b : P * (b + 1)], gb_col[:, b : b + 1].to_broadcast([P, P]), ident_bf[:])
            nc.tensor.transpose(
                beta_ps[:, P * b : P * (b + 1)], gb_col[:, F_BLOCKS + b : F_BLOCKS + b + 1].to_broadcast([P, P]), ident_bf[:]
            )
        spread.extend([gamma_ps, beta_ps])
        while steps[-1] < len(order) + ALAG or finished or measured or scaled:
            step()
